import numpy as np
import ml_dtypes


def mxq(x, axis, fmt="e4m3"):
    dtype, down = {"e4m3": (ml_dtypes.float8_e4m3fn, 7), "e5m2": (ml_dtypes.float8_e5m2, 14)}[fmt]
    v = np.moveaxis(np.asarray(x, np.float32).astype(ml_dtypes.bfloat16).astype(np.float64), axis, -1)
    blocks = v.reshape(v.shape[:-1] + (-1, 32))
    amax = np.abs(blocks).max(-1, keepdims=True)
    byte = np.maximum(np.where(amax > 0, np.frexp(amax)[1] - 1 + 127, 0) - down, 1)
    scale = np.exp2(byte - 127.0)
    codes = (blocks / scale).astype(np.float32).astype(dtype).astype(np.float64)
    return np.moveaxis((codes * scale).reshape(v.shape), -1, axis)


WIDE = False


def mx_kscale(k):
    if not WIDE:
        return np.ones(k)
    levels = np.array([10, -10, 5, -5, 0])
    a = np.random.permutation(np.resize(levels, k // 512 * 4)).reshape(k // 512, 4)
    idx = np.arange(k)
    return np.exp2(a[idx // 512, idx % 128 // 32])


BF16 = ml_dtypes.bfloat16


def bf(x):
    return np.asarray(x, np.float32).astype(BF16)


def f64(x):
    return np.asarray(x).astype(np.float64)


E2M1 = np.array([0.0, 0.5, 1.0, 1.5, 2.0, 3.0, 4.0, 6.0, -0.0, -0.5, -1.0, -1.5, -2.0, -3.0, -4.0, -6.0])


def pack_weight(w, fmt):
    k, n = w.shape
    w = f64(bf(w)).reshape(k // 32, 32, n)
    amax = np.abs(w).max(1)
    if fmt == "e4m3":
        byte = np.frexp(amax)[1] - 1 + 127 - 7
    else:
        mant, ex = np.frexp(amax / 6.0)
        byte = np.where(mant > 0.5, ex, ex - 1) + 127
    byte = np.clip(np.where(amax > 0, byte, 1), 1, 254)
    scaled = (w * np.exp2(127.0 - byte)[:, None, :]).reshape(k, n).astype(np.float32)
    by_word = np.ascontiguousarray(scaled.reshape(k // 512, 128, 4, n).transpose(0, 1, 3, 2))
    if fmt == "e4m3":
        words = by_word.astype(ml_dtypes.float8_e4m3fn).view(np.uint8)
    else:
        c = by_word.astype(ml_dtypes.float4_e2m1fn).view(np.uint8) & 0xF
        words = c[..., 0::2] | (c[..., 1::2] << 4)
    return np.ascontiguousarray(words), np.ascontiguousarray(byte.astype(np.uint8).reshape(k // 512, 16, n))


def unpack_weight(words, scales, fmt):
    g, p, n, _ = words.shape
    if fmt == "e4m3":
        vals = np.ascontiguousarray(words).view(ml_dtypes.float8_e4m3fn).astype(np.float64)
    else:
        nib = np.empty((g, p, n, 4), np.uint8)
        nib[..., 0::2] = words & 0xF
        nib[..., 1::2] = words >> 4
        vals = E2M1[nib]
    vals = vals * np.repeat(np.exp2(scales.astype(np.float64) - 127.0), 8, axis=1)[..., None]
    return vals.transpose(0, 1, 3, 2).reshape(g * 512, n)


B, N, D_IN, H, D_HEAD, D_EXPAND = 4, 1024, 512, 1, 128, 512
D_V = D_IN * H
EPS = 1e-5


def feature_norm(x, gamma, beta):
    mean = x.mean(axis=1, keepdims=True)
    var = x.var(axis=1, keepdims=True)
    return gamma * (x - mean) / np.sqrt(var + EPS) + beta


def setup_inputs():
    t = mx_kscale(D_V)
    s = mx_kscale(D_IN)
    attn_out = bf(5.0 * np.random.standard_normal((B, N, D_V)) * t)
    x = bf(1.5 * np.random.standard_normal((B, N, D_IN)))
    W_merge_words, W_merge_scales = pack_weight(np.random.standard_normal((D_V, D_IN)) * 0.2 / np.sqrt(D_V) / t[:, None], "e4m3")
    b_merge = bf(0.3 * np.random.standard_normal(D_IN))
    gamma2 = bf((1.0 + 0.1 * np.random.standard_normal((1, 1, D_IN))) * s)
    beta2 = bf(0.2 * np.random.standard_normal((1, 1, D_IN)) * s)
    W1_words, W1_scales = pack_weight(np.random.standard_normal((D_IN, D_EXPAND)) / np.sqrt(D_IN) / s[:, None], "e4m3")
    b1 = bf(0.2 * np.random.standard_normal(D_EXPAND))
    return {"attn_out": attn_out,
            "x": x,
            "W_merge_words": W_merge_words,
            "W_merge_scales": W_merge_scales,
            "b_merge": b_merge,
            "gamma2": gamma2,
            "beta2": beta2,
            "W1_words": W1_words,
            "W1_scales": W1_scales,
            "b1": b1}


def reference(attn_out, x, W_merge_words, W_merge_scales, b_merge, gamma2, beta2, W1_words, W1_scales, b1):
    x2 = f64(x) + (mxq(f64(attn_out), 2, "e4m3") @ unpack_weight(W_merge_words, W_merge_scales, "e4m3")) + f64(b_merge)
    xn = feature_norm(x2, f64(gamma2), f64(beta2))
    ffh = (mxq(xn, 2, "e4m3") @ unpack_weight(W1_words, W1_scales, "e4m3")) + f64(b1)
    return x2, ffh

@@ -1,0 +1,252 @@
+import concourse.mybir as mybir
+from concourse.masks import make_identity
+
+FLOPS = 2 * 2 * 4096 * 512 * 512
+
+FP8X4 = mybir.dt.float8_e4m3fn_x4
+BF16 = mybir.dt.bfloat16
+F32 = mybir.dt.float32
+I32 = mybir.dt.int32
+U32 = mybir.dt.uint32
+U8 = mybir.dt.uint8
+ACT = mybir.ActivationFunctionType
+ALU = mybir.AluOpType
+AXIS = mybir.AxisListType
+
+P = 128
+PACK = 4
+D = P * PACK
+BATCH = 4
+TOKENS = 1024
+TILES = 4
+CHUNK = TILES * P
+HALVES = TOKENS // CHUNK
+N_CHUNKS = BATCH * HALVES
+NORM_LAG = HALVES
+EPS = 1e-5
+
+
+def load_weight(nc, pool, words_dram, scales_dram, label):
+    words = pool.tile([P, D], U32, name=label + "_words", align_bytes=64)
+    plane = pool.tile([P, D], U8, name=label + "_plane", align_bytes=64)
+    nc.vector.memset(plane[:].bitcast(I32), 0)
+    for quadrant in range(4):
+        nc.sync.dma_start(
+            out=plane[32 * quadrant : 32 * quadrant + 4, :].bitcast(I32),
+            in_=scales_dram[0, 4 * quadrant : 4 * quadrant + 4, :].bitcast(I32),
+        )
+    nc.sync.dma_start(out=words[:].bitcast(I32), in_=words_dram[0].rearrange("p n t -> p (n t)").bitcast(I32))
+    return words, plane
+
+
+def tile_attentionblock_pc_t_kernel(
+    tc, attn_out, x, W_merge_words, W_merge_scales, b_merge, gamma2, beta2, W1_words, W1_scales, b1, out_0, out_1
+):
+    nc = tc.nc
+    attn_rows = attn_out.rearrange("b (p i) k -> b p (i k)", p=P)
+    x_rows = x.rearrange("b (p i) k -> b p (i k)", p=P)
+    x2_rows = out_0.rearrange("b (p i) n -> b p (i n)", p=P)
+    ffh_rows = out_1.rearrange("b (p i) n -> b p (i n)", p=P)
+
+    with (
+        tc.tile_pool(name="keep", bufs=1) as keep,
+        tc.tile_pool(name="work", bufs=2) as work,
+        tc.psum_pool(name="attn_t", bufs=2) as attn_t_pool,
+        tc.psum_pool(name="product", bufs=3) as product_pool,
+        tc.psum_pool(name="y_t", bufs=3) as y_t_pool,
+    ):
+        attn_all = keep.tile([P, N_CHUNKS, TILES * D], BF16)
+        x_all = keep.tile([P, N_CHUNKS, TILES * D], BF16)
+
+        def load_chunk(rows, resident, c):
+            batch, half = divmod(c, HALVES)
+            nc.sync.dma_start(out=resident[:, c, :], in_=rows[batch][:, half * TILES * D : (half + 1) * TILES * D])
+
+        load_chunk(attn_rows, attn_all, 0)
+        merge_words, merge_plane = load_weight(nc, keep, W_merge_words, W_merge_scales, "merge")
+        load_chunk(x_rows, x_all, 0)
+        load_chunk(attn_rows, attn_all, 1)
+        load_chunk(x_rows, x_all, 1)
+        w1_words, w1_plane = load_weight(nc, keep, W1_words, W1_scales, "w1")
+        for c in range(2, N_CHUNKS):
+            load_chunk(attn_rows, attn_all, c)
+            load_chunk(x_rows, x_all, c)
+
+        b_merge_rows = keep.tile([P, D], BF16)
+        nc.scalar.dma_start(out=b_merge_rows[:], in_=b_merge.partition_broadcast(P))
+        b1_rows = keep.tile([P, D], BF16)
+        nc.scalar.dma_start(out=b1_rows[:], in_=b1.partition_broadcast(P))
+        gamma_pt = keep.tile([P, PACK], BF16)
+        nc.scalar.dma_start(out=gamma_pt[:], in_=gamma2.rearrange("a b (p t) -> (a b p) t", t=PACK))
+        beta_pt = keep.tile([P, PACK], BF16)
+        nc.scalar.dma_start(out=beta_pt[:], in_=beta2.rearrange("a b (p t) -> (a b p) t", t=PACK))
+
+        identity = keep.tile([P, P], F32)
+        make_identity(nc, identity[:])
+
+        one = keep.tile([P, 1], F32)
+        nc.vector.memset(one[:], 1.0)
+        nc.scalar.sqrt(out=one[:], in_=one[:])
+
+        attn_mx = {}
+        xn_mx = {}
+        y_of_chunk = {}
+        y_t_of_batch = {}
+        sums_of_batch = {}
+        norm_of_batch = {}
+
+        def chunk_columns(c):
+            half = c % HALVES
+            return slice(half * TILES * D, (half + 1) * TILES * D)
+
+        def transpose_attn(c):
+            attn_words = attn_all[:, c, :].bitcast(F32)
+            attn_grouped = work.tile([P, CHUNK * PACK], BF16, align_bytes=64)
+            grouped_words = attn_grouped[:].bitcast(F32).rearrange("p (i w u) -> p i w u", i=TILES, u=2)
+            for pair in range(TILES // 2):
+                attn_t = attn_t_pool.tile([P, 2, 2, P], F32)
+                for j in range(2):
+                    first_word = (2 * pair + j) * (D // 2)
+                    for u in range(2):
+                        nc.tensor.transpose(
+                            attn_t[:, j, u, :], attn_words[:, first_word + u : first_word + D // 2 : 2], identity[:]
+                        )
+                nc.scalar.copy(
+                    out=grouped_words[:, 2 * pair : 2 * pair + 2], in_=attn_t[:].rearrange("p j u w -> p j w u")
+                )
+            return attn_grouped
+
+        def quantise(grouped, label):
+            codes = work.tile([P, CHUNK], U32, name=label + "_codes", align_bytes=64)
+            plane = work.tile([P, CHUNK], U8, name=label + "_plane", align_bytes=64)
+            nc.vector.quantize_mx(out=codes[:].bitcast(FP8X4), scales=plane[:], in_=grouped)
+            return codes, plane
+
+        def product_of(activation_mx, i, weight_words, weight_plane):
+            codes, plane = activation_mx
+            tokens = slice(i * P, (i + 1) * P)
+            product = product_pool.tile([P, D], F32)
+            nc.tensor.matmul_mx(
+                out=product[:],
+                lhsT=codes[:, tokens].bitcast(FP8X4),
+                lhsT_scale=plane[:, tokens],
+                rhs=weight_words[:].bitcast(FP8X4),
+                rhs_scale=weight_plane[:],
+                start=True,
+                stop=True,
+            )
+            return product
+
+        def merge(c):
+            y = work.tile([P, TILES, D], F32, bufs=3)
+            y_of_chunk[c] = y
+            x2 = work.tile([P, TILES, D], F32, bufs=3)
+            for i in range(TILES):
+                product = product_of(attn_mx[c], i, merge_words, merge_plane)
+                nc.vector.tensor_tensor(out=y[:, i, :], in0=product[:], in1=x_all[:, c, i * D : (i + 1) * D], op=ALU.add)
+                nc.gpsimd.tensor_tensor(out=x2[:, i, :], in0=y[:, i, :], in1=b_merge_rows[:], op=ALU.add)
+            nc.sync.dma_start(out=x2_rows[c // HALVES][:, chunk_columns(c)], in_=x2[:].rearrange("p i n -> p (i n)"))
+
+        def transpose_y(c):
+            batch, half = divmod(c, HALVES)
+            if half == 0:
+                y_t_all = work.tile([P, PACK, TOKENS], F32)
+                y_t_of_batch[batch] = y_t_all
+                sums = work.tile([P, 2, PACK, HALVES], F32)
+                sums_of_batch[batch] = sums
+            y = y_of_chunk[c]
+            for t in range(PACK):
+                y_t = y_t_pool.tile([P, TILES, P], F32)
+                for i in range(TILES):
+                    nc.tensor.transpose(y_t[:, i, :], y[:, i, t:D:PACK], identity[:])
+                nc.scalar.activation(
+                    out=y_t_of_batch[batch][:, t, half * CHUNK : (half + 1) * CHUNK],
+                    in_=y_t[:].rearrange("p i w -> p (i w)"),
+                    func=ACT.Identity,
+                    accum_out=sums_of_batch[batch][:, 0, t, half : half + 1],
+                )
+                squares = work.tile([P, CHUNK], BF16, bufs=4)
+                nc.scalar.activation(
+                    out=squares[:],
+                    in_=y_t[:].rearrange("p i w -> p (i w)"),
+                    func=ACT.Square,
+                    accum_out=sums_of_batch[batch][:, 1, t, half : half + 1],
+                )
+
+        def norm_coefficients(batch):
+            totals = work.tile([P, 2 * PACK], F32)
+            nc.vector.tensor_reduce(
+                out=totals[:], in_=sums_of_batch[batch][:].rearrange("p k t h -> p (k t) h"), axis=AXIS.X, op=ALU.add
+            )
+            moments = work.tile([P, 2, PACK], F32)
+            nc.vector.tensor_scalar_mul(moments[:].rearrange("p k t -> p (k t)"), totals[:], 1.0 / TOKENS)
+            mean = moments[:, 0, :]
+            mean_squared = work.tile([P, PACK], F32)
+            nc.vector.tensor_mul(mean_squared[:], mean, mean)
+            var_eps = work.tile([P, PACK], F32)
+            nc.vector.scalar_tensor_tensor(
+                out=var_eps[:], in0=moments[:, 1, :], scalar=EPS, in1=mean_squared[:], op0=ALU.add, op1=ALU.subtract
+            )
+            std = work.tile([P, PACK], F32)
+            nc.scalar.sqrt(out=std[:], in_=var_eps[:])
+            rstd = work.tile([P, PACK], F32)
+            nc.vector.reciprocal(rstd[:], std[:])
+            gain = work.tile([P, PACK], F32)
+            nc.vector.tensor_mul(gain[:], gamma_pt[:], rstd[:])
+            mean_gain = work.tile([P, PACK], F32)
+            nc.vector.tensor_mul(mean_gain[:], mean, gain[:])
+            shift = work.tile([P, PACK], F32)
+            nc.vector.tensor_sub(shift[:], beta_pt[:], mean_gain[:])
+            norm_of_batch[batch] = (gain, shift)
+
+        def normalise(c):
+            batch, half = divmod(c, HALVES)
+            gain, shift = norm_of_batch[batch]
+            xn_planes = work.tile([P, PACK, CHUNK], BF16)
+            for t in range(PACK):
+                y_t_plane = y_t_of_batch[batch][:, t, half * CHUNK : (half + 1) * CHUNK]
+                if t < PACK // 2:
+                    nc.scalar.activation(
+                        out=xn_planes[:, t, :],
+                        in_=y_t_plane,
+                        func=ACT.Identity,
+                        scale=gain[:, t : t + 1],
+                        bias=shift[:, t : t + 1],
+                    )
+                else:
+                    nc.vector.tensor_scalar(
+                        out=xn_planes[:, t, :],
+                        in0=y_t_plane,
+                        scalar1=gain[:, t : t + 1],
+                        scalar2=shift[:, t : t + 1],
+                        op0=ALU.mult,
+                        op1=ALU.add,
+                    )
+            xn_grouped = work.tile([P, CHUNK, PACK], BF16, align_bytes=64)
+            nc.vector.tensor_copy(out=xn_grouped[:], in_=xn_planes[:].rearrange("p t w -> p w t"))
+            return xn_grouped
+
+        def expand(c):
+            ffh = work.tile([P, TILES, D], F32, bufs=3)
+            for i in range(TILES):
+                product = product_of(xn_mx[c], i, w1_words, w1_plane)
+                nc.vector.tensor_tensor(out=ffh[:, i, :], in0=product[:], in1=b1_rows[:], op=ALU.add)
+            nc.sync.dma_start(out=ffh_rows[c // HALVES][:, chunk_columns(c)], in_=ffh[:].rearrange("p i n -> p (i n)"))
+
+        chunks = range(N_CHUNKS)
+        for step in range(-1, N_CHUNKS + NORM_LAG + 1):
+            if step - NORM_LAG in chunks and (step - NORM_LAG) % HALVES == 0:
+                norm_coefficients((step - NORM_LAG) // HALVES)
+            if step + 1 in chunks:
+                attn_grouped = transpose_attn(step + 1)
+            if step in chunks:
+                merge(step)
+            if step + 1 in chunks:
+                attn_mx[step + 1] = quantise(attn_grouped[:], "attn")
+            if step - NORM_LAG in chunks:
+                xn_grouped = normalise(step - NORM_LAG)
+                xn_mx[step - NORM_LAG] = quantise(xn_grouped[:].rearrange("p w t -> p (w t)"), "xn")
+            if step in chunks:
+                transpose_y(step)
+            if step - NORM_LAG - 1 in chunks:
+                expand(step - NORM_LAG - 1)

@@ -49,6 +49,7 @@ def tile_attentionblock_pc_t_kernel(
     ffh_rows = out_1.rearrange("b (p i) n -> b p (i n)", p=P)
 
     with (
+        tc.manual_schedule(),
         tc.tile_pool(name="keep", bufs=1) as keep,
         tc.tile_pool(name="work", bufs=2) as work,
         tc.psum_pool(name="attn_t", bufs=2) as attn_t_pool,
@@ -88,9 +89,11 @@ def tile_attentionblock_pc_t_kernel(
         nc.vector.memset(one[:], 1.0)
         nc.scalar.sqrt(out=one[:], in_=one[:])
 
+        attn_t_of_chunk = {}
         attn_mx = {}
         xn_mx = {}
         y_of_chunk = {}
+        y_t_bank = {}
         y_t_of_batch = {}
         sums_of_batch = {}
         norm_of_batch = {}
@@ -101,8 +104,7 @@ def tile_attentionblock_pc_t_kernel(
 
         def transpose_attn(c):
             attn_words = attn_all[:, c, :].bitcast(F32)
-            attn_grouped = work.tile([P, CHUNK * PACK], BF16, align_bytes=64)
-            grouped_words = attn_grouped[:].bitcast(F32).rearrange("p (i w u) -> p i w u", i=TILES, u=2)
+            banks = []
             for pair in range(TILES // 2):
                 attn_t = attn_t_pool.tile([P, 2, 2, P], F32)
                 for j in range(2):
@@ -111,8 +113,16 @@ def tile_attentionblock_pc_t_kernel(
                         nc.tensor.transpose(
                             attn_t[:, j, u, :], attn_words[:, first_word + u : first_word + D // 2 : 2], identity[:]
                         )
+                banks.append(attn_t)
+            attn_t_of_chunk[c] = banks
+
+        def group_attn(c):
+            attn_grouped = work.tile([P, CHUNK * PACK], BF16, align_bytes=64)
+            grouped_words = attn_grouped[:].bitcast(F32).rearrange("p (i w u) -> p i w u", i=TILES, u=2)
+            for pair in range(TILES // 2):
                 nc.scalar.copy(
-                    out=grouped_words[:, 2 * pair : 2 * pair + 2], in_=attn_t[:].rearrange("p j u w -> p j w u")
+                    out=grouped_words[:, 2 * pair : 2 * pair + 2],
+                    in_=attn_t_of_chunk[c][pair][:].rearrange("p j u w -> p j w u"),
                 )
             return attn_grouped
 
@@ -147,31 +157,30 @@ def tile_attentionblock_pc_t_kernel(
                 nc.gpsimd.tensor_tensor(out=x2[:, i, :], in0=y[:, i, :], in1=b_merge_rows[:], op=ALU.add)
             nc.sync.dma_start(out=x2_rows[c // HALVES][:, chunk_columns(c)], in_=x2[:].rearrange("p i n -> p (i n)"))
 
-        def transpose_y(c):
+        def transpose_y(c, t):
+            y_t = y_t_pool.tile([P, TILES, P], F32)
+            for i in range(TILES):
+                nc.tensor.transpose(y_t[:, i, :], y_of_chunk[c][:, i, t:D:PACK], identity[:])
+            y_t_bank[c, t] = y_t
+
+        def keep_and_sum_y(c, t):
             batch, half = divmod(c, HALVES)
-            if half == 0:
+            if half == 0 and t == 0:
                 y_t_all = work.tile([P, PACK, TOKENS], F32)
                 y_t_of_batch[batch] = y_t_all
                 sums = work.tile([P, 2, PACK, HALVES], F32)
                 sums_of_batch[batch] = sums
-            y = y_of_chunk[c]
-            for t in range(PACK):
-                y_t = y_t_pool.tile([P, TILES, P], F32)
-                for i in range(TILES):
-                    nc.tensor.transpose(y_t[:, i, :], y[:, i, t:D:PACK], identity[:])
-                nc.scalar.activation(
-                    out=y_t_of_batch[batch][:, t, half * CHUNK : (half + 1) * CHUNK],
-                    in_=y_t[:].rearrange("p i w -> p (i w)"),
-                    func=ACT.Identity,
-                    accum_out=sums_of_batch[batch][:, 0, t, half : half + 1],
-                )
-                squares = work.tile([P, CHUNK], BF16, bufs=4)
-                nc.scalar.activation(
-                    out=squares[:],
-                    in_=y_t[:].rearrange("p i w -> p (i w)"),
-                    func=ACT.Square,
-                    accum_out=sums_of_batch[batch][:, 1, t, half : half + 1],
-                )
+            plane = y_t_bank[c, t][:].rearrange("p i w -> p (i w)")
+            nc.scalar.activation(
+                out=y_t_of_batch[batch][:, t, half * CHUNK : (half + 1) * CHUNK],
+                in_=plane,
+                func=ACT.Identity,
+                accum_out=sums_of_batch[batch][:, 0, t, half : half + 1],
+            )
+            squares = work.tile([P, CHUNK], BF16, bufs=4)
+            nc.scalar.activation(
+                out=squares[:], in_=plane, func=ACT.Square, accum_out=sums_of_batch[batch][:, 1, t, half : half + 1]
+            )
 
         def norm_coefficients(batch):
             totals = work.tile([P, 2 * PACK], F32)
@@ -222,6 +231,9 @@ def tile_attentionblock_pc_t_kernel(
                         op0=ALU.mult,
                         op1=ALU.add,
                     )
+            return xn_planes
+
+        def group_xn(xn_planes):
             xn_grouped = work.tile([P, CHUNK, PACK], BF16, align_bytes=64)
             nc.vector.tensor_copy(out=xn_grouped[:], in_=xn_planes[:].rearrange("p t w -> p w t"))
             return xn_grouped
@@ -234,19 +246,33 @@ def tile_attentionblock_pc_t_kernel(
             nc.sync.dma_start(out=ffh_rows[c // HALVES][:, chunk_columns(c)], in_=ffh[:].rearrange("p i n -> p (i n)"))
 
         chunks = range(N_CHUNKS)
-        for step in range(-1, N_CHUNKS + NORM_LAG + 1):
-            if step - NORM_LAG in chunks and (step - NORM_LAG) % HALVES == 0:
-                norm_coefficients((step - NORM_LAG) // HALVES)
-            if step + 1 in chunks:
-                attn_grouped = transpose_attn(step + 1)
+        for step in range(-2, N_CHUNKS + NORM_LAG + 1):
+            ahead, normed, expanded = step + 1, step - NORM_LAG, step - NORM_LAG - 1
+            if ahead in chunks:
+                attn_grouped = group_attn(ahead)
             if step in chunks:
                 merge(step)
-            if step + 1 in chunks:
-                attn_mx[step + 1] = quantise(attn_grouped[:], "attn")
-            if step - NORM_LAG in chunks:
-                xn_grouped = normalise(step - NORM_LAG)
-                xn_mx[step - NORM_LAG] = quantise(xn_grouped[:].rearrange("p w t -> p (w t)"), "xn")
+            if normed in chunks and normed % HALVES == 0:
+                norm_coefficients(normed // HALVES)
+            if ahead in chunks:
+                attn_mx[ahead] = quantise(attn_grouped[:], "attn")
             if step in chunks:
-                transpose_y(step)
-            if step - NORM_LAG - 1 in chunks:
-                expand(step - NORM_LAG - 1)
+                transpose_y(step, 0)
+            if expanded in chunks:
+                expand(expanded)
+            if step in chunks:
+                keep_and_sum_y(step, 0)
+                transpose_y(step, 1)
+                transpose_y(step, 2)
+            if ahead + 1 in chunks:
+                transpose_attn(ahead + 1)
+            if normed in chunks:
+                xn_planes = normalise(normed)
+            if step in chunks:
+                keep_and_sum_y(step, 1)
+                transpose_y(step, 3)
+                keep_and_sum_y(step, 2)
+                keep_and_sum_y(step, 3)
+            if normed in chunks:
+                xn_grouped = group_xn(xn_planes)
+                xn_mx[normed] = quantise(xn_grouped[:].rearrange("p w t -> p (w t)"), "xn")

@@ -49,7 +49,6 @@ def tile_attentionblock_pc_t_kernel(
     ffh_rows = out_1.rearrange("b (p i) n -> b p (i n)", p=P)
 
     with (
-        tc.manual_schedule(),
         tc.tile_pool(name="keep", bufs=1) as keep,
         tc.tile_pool(name="work", bufs=2) as work,
         tc.psum_pool(name="attn_t", bufs=2) as attn_t_pool,
@@ -89,11 +88,9 @@ def tile_attentionblock_pc_t_kernel(
         nc.vector.memset(one[:], 1.0)
         nc.scalar.sqrt(out=one[:], in_=one[:])
 
-        attn_t_of_chunk = {}
         attn_mx = {}
         xn_mx = {}
         y_of_chunk = {}
-        y_t_bank = {}
         y_t_of_batch = {}
         sums_of_batch = {}
         norm_of_batch = {}
@@ -104,7 +101,8 @@ def tile_attentionblock_pc_t_kernel(
 
         def transpose_attn(c):
             attn_words = attn_all[:, c, :].bitcast(F32)
-            banks = []
+            attn_grouped = work.tile([P, CHUNK * PACK], BF16, align_bytes=64)
+            grouped_words = attn_grouped[:].bitcast(F32).rearrange("p (i w u) -> p i w u", i=TILES, u=2)
             for pair in range(TILES // 2):
                 attn_t = attn_t_pool.tile([P, 2, 2, P], F32)
                 for j in range(2):
@@ -113,16 +111,8 @@ def tile_attentionblock_pc_t_kernel(
                         nc.tensor.transpose(
                             attn_t[:, j, u, :], attn_words[:, first_word + u : first_word + D // 2 : 2], identity[:]
                         )
-                banks.append(attn_t)
-            attn_t_of_chunk[c] = banks
-
-        def group_attn(c):
-            attn_grouped = work.tile([P, CHUNK * PACK], BF16, align_bytes=64)
-            grouped_words = attn_grouped[:].bitcast(F32).rearrange("p (i w u) -> p i w u", i=TILES, u=2)
-            for pair in range(TILES // 2):
                 nc.scalar.copy(
-                    out=grouped_words[:, 2 * pair : 2 * pair + 2],
-                    in_=attn_t_of_chunk[c][pair][:].rearrange("p j u w -> p j w u"),
+                    out=grouped_words[:, 2 * pair : 2 * pair + 2], in_=attn_t[:].rearrange("p j u w -> p j w u")
                 )
             return attn_grouped
 
@@ -154,33 +144,34 @@ def tile_attentionblock_pc_t_kernel(
             for i in range(TILES):
                 product = product_of(attn_mx[c], i, merge_words, merge_plane)
                 nc.vector.tensor_tensor(out=y[:, i, :], in0=product[:], in1=x_all[:, c, i * D : (i + 1) * D], op=ALU.add)
-                nc.gpsimd.tensor_tensor(out=x2[:, i, :], in0=y[:, i, :], in1=b_merge_rows[:], op=ALU.add)
+                nc.vector.tensor_tensor(out=x2[:, i, :], in0=y[:, i, :], in1=b_merge_rows[:], op=ALU.add)
             nc.sync.dma_start(out=x2_rows[c // HALVES][:, chunk_columns(c)], in_=x2[:].rearrange("p i n -> p (i n)"))
 
-        def transpose_y(c, t):
-            y_t = y_t_pool.tile([P, TILES, P], F32)
-            for i in range(TILES):
-                nc.tensor.transpose(y_t[:, i, :], y_of_chunk[c][:, i, t:D:PACK], identity[:])
-            y_t_bank[c, t] = y_t
-
-        def keep_and_sum_y(c, t):
+        def transpose_y(c):
             batch, half = divmod(c, HALVES)
-            if half == 0 and t == 0:
+            if half == 0:
                 y_t_all = work.tile([P, PACK, TOKENS], F32)
                 y_t_of_batch[batch] = y_t_all
                 sums = work.tile([P, 2, PACK, HALVES], F32)
                 sums_of_batch[batch] = sums
-            plane = y_t_bank[c, t][:].rearrange("p i w -> p (i w)")
-            nc.scalar.activation(
-                out=y_t_of_batch[batch][:, t, half * CHUNK : (half + 1) * CHUNK],
-                in_=plane,
-                func=ACT.Identity,
-                accum_out=sums_of_batch[batch][:, 0, t, half : half + 1],
-            )
-            squares = work.tile([P, CHUNK], BF16, bufs=4)
-            nc.scalar.activation(
-                out=squares[:], in_=plane, func=ACT.Square, accum_out=sums_of_batch[batch][:, 1, t, half : half + 1]
-            )
+            y = y_of_chunk[c]
+            for t in range(PACK):
+                y_t = y_t_pool.tile([P, TILES, P], F32)
+                for i in range(TILES):
+                    nc.tensor.transpose(y_t[:, i, :], y[:, i, t:D:PACK], identity[:])
+                nc.scalar.activation(
+                    out=y_t_of_batch[batch][:, t, half * CHUNK : (half + 1) * CHUNK],
+                    in_=y_t[:].rearrange("p i w -> p (i w)"),
+                    func=ACT.Identity,
+                    accum_out=sums_of_batch[batch][:, 0, t, half : half + 1],
+                )
+                squares = work.tile([P, CHUNK], BF16, bufs=4)
+                nc.scalar.activation(
+                    out=squares[:],
+                    in_=y_t[:].rearrange("p i w -> p (i w)"),
+                    func=ACT.Square,
+                    accum_out=sums_of_batch[batch][:, 1, t, half : half + 1],
+                )
 
         def norm_coefficients(batch):
             totals = work.tile([P, 2 * PACK], F32)
@@ -231,9 +222,6 @@ def tile_attentionblock_pc_t_kernel(
                         op0=ALU.mult,
                         op1=ALU.add,
                     )
-            return xn_planes
-
-        def group_xn(xn_planes):
             xn_grouped = work.tile([P, CHUNK, PACK], BF16, align_bytes=64)
             nc.vector.tensor_copy(out=xn_grouped[:], in_=xn_planes[:].rearrange("p t w -> p w t"))
             return xn_grouped
@@ -246,33 +234,19 @@ def tile_attentionblock_pc_t_kernel(
             nc.sync.dma_start(out=ffh_rows[c // HALVES][:, chunk_columns(c)], in_=ffh[:].rearrange("p i n -> p (i n)"))
 
         chunks = range(N_CHUNKS)
-        for step in range(-2, N_CHUNKS + NORM_LAG + 1):
-            ahead, normed, expanded = step + 1, step - NORM_LAG, step - NORM_LAG - 1
-            if ahead in chunks:
-                attn_grouped = group_attn(ahead)
+        for step in range(-1, N_CHUNKS + NORM_LAG + 1):
+            if step - NORM_LAG in chunks and (step - NORM_LAG) % HALVES == 0:
+                norm_coefficients((step - NORM_LAG) // HALVES)
+            if step + 1 in chunks:
+                attn_grouped = transpose_attn(step + 1)
             if step in chunks:
                 merge(step)
-            if normed in chunks and normed % HALVES == 0:
-                norm_coefficients(normed // HALVES)
-            if ahead in chunks:
-                attn_mx[ahead] = quantise(attn_grouped[:], "attn")
+            if step + 1 in chunks:
+                attn_mx[step + 1] = quantise(attn_grouped[:], "attn")
+            if step - NORM_LAG in chunks:
+                xn_grouped = normalise(step - NORM_LAG)
+                xn_mx[step - NORM_LAG] = quantise(xn_grouped[:].rearrange("p w t -> p (w t)"), "xn")
             if step in chunks:
-                transpose_y(step, 0)
-            if expanded in chunks:
-                expand(expanded)
-            if step in chunks:
-                keep_and_sum_y(step, 0)
-                transpose_y(step, 1)
-                transpose_y(step, 2)
-            if ahead + 1 in chunks:
-                transpose_attn(ahead + 1)
-            if normed in chunks:
-                xn_planes = normalise(normed)
-            if step in chunks:
-                keep_and_sum_y(step, 1)
-                transpose_y(step, 3)
-                keep_and_sum_y(step, 2)
-                keep_and_sum_y(step, 3)
-            if normed in chunks:
-                xn_grouped = group_xn(xn_planes)
-                xn_mx[normed] = quantise(xn_grouped[:].rearrange("p w t -> p (w t)"), "xn")
+                transpose_y(step)
+            if step - NORM_LAG - 1 in chunks:
+                expand(step - NORM_LAG - 1)

@@ -53,7 +53,7 @@ def tile_attentionblock_pc_t_kernel(
         tc.tile_pool(name="work", bufs=2) as work,
         tc.psum_pool(name="attn_t", bufs=2) as attn_t_pool,
         tc.psum_pool(name="product", bufs=3) as product_pool,
-        tc.psum_pool(name="y_t", bufs=3) as y_t_pool,
+        tc.psum_pool(name="x2_t", bufs=3) as x2_t_pool,
     ):
         attn_all = keep.tile([P, N_CHUNKS, TILES * D], BF16)
         x_all = keep.tile([P, N_CHUNKS, TILES * D], BF16)
@@ -72,8 +72,17 @@ def tile_attentionblock_pc_t_kernel(
             load_chunk(attn_rows, attn_all, c)
             load_chunk(x_rows, x_all, c)
 
+        identity = keep.tile([P, P], F32)
+        make_identity(nc, identity[:])
+
         b_merge_rows = keep.tile([P, D], BF16)
         nc.scalar.dma_start(out=b_merge_rows[:], in_=b_merge.partition_broadcast(P))
+        x2_all = keep.tile([P, N_CHUNKS, TILES * D], F32)
+        for c in range(N_CHUNKS):
+            adder = nc.gpsimd if c < N_CHUNKS // 2 else nc.vector
+            for i in range(TILES):
+                features = slice(i * D, (i + 1) * D)
+                adder.tensor_tensor(out=x2_all[:, c, features], in0=x_all[:, c, features], in1=b_merge_rows[:], op=ALU.add)
         b1_rows = keep.tile([P, D], BF16)
         nc.scalar.dma_start(out=b1_rows[:], in_=b1.partition_broadcast(P))
         gamma_pt = keep.tile([P, PACK], BF16)
@@ -81,17 +90,13 @@ def tile_attentionblock_pc_t_kernel(
         beta_pt = keep.tile([P, PACK], BF16)
         nc.scalar.dma_start(out=beta_pt[:], in_=beta2.rearrange("a b (p t) -> (a b p) t", t=PACK))
 
-        identity = keep.tile([P, P], F32)
-        make_identity(nc, identity[:])
-
         one = keep.tile([P, 1], F32)
         nc.vector.memset(one[:], 1.0)
         nc.scalar.sqrt(out=one[:], in_=one[:])
 
         attn_mx = {}
         xn_mx = {}
-        y_of_chunk = {}
-        y_t_of_batch = {}
+        x2_t_of_batch = {}
         sums_of_batch = {}
         norm_of_batch = {}
 
@@ -138,37 +143,33 @@ def tile_attentionblock_pc_t_kernel(
             return product
 
         def merge(c):
-            y = work.tile([P, TILES, D], F32, bufs=3)
-            y_of_chunk[c] = y
-            x2 = work.tile([P, TILES, D], F32, bufs=3)
             for i in range(TILES):
+                features = slice(i * D, (i + 1) * D)
                 product = product_of(attn_mx[c], i, merge_words, merge_plane)
-                nc.vector.tensor_tensor(out=y[:, i, :], in0=product[:], in1=x_all[:, c, i * D : (i + 1) * D], op=ALU.add)
-                nc.vector.tensor_tensor(out=x2[:, i, :], in0=y[:, i, :], in1=b_merge_rows[:], op=ALU.add)
-            nc.sync.dma_start(out=x2_rows[c // HALVES][:, chunk_columns(c)], in_=x2[:].rearrange("p i n -> p (i n)"))
+                nc.vector.tensor_tensor(out=x2_all[:, c, features], in0=product[:], in1=x2_all[:, c, features], op=ALU.add)
+            nc.sync.dma_start(out=x2_rows[c // HALVES][:, chunk_columns(c)], in_=x2_all[:, c, :])
 
-        def transpose_y(c):
+        def transpose_x2(c):
             batch, half = divmod(c, HALVES)
             if half == 0:
-                y_t_all = work.tile([P, PACK, TOKENS], F32)
-                y_t_of_batch[batch] = y_t_all
+                x2_t_all = work.tile([P, PACK, TOKENS], F32)
+                x2_t_of_batch[batch] = x2_t_all
                 sums = work.tile([P, 2, PACK, HALVES], F32)
                 sums_of_batch[batch] = sums
-            y = y_of_chunk[c]
             for t in range(PACK):
-                y_t = y_t_pool.tile([P, TILES, P], F32)
+                x2_t = x2_t_pool.tile([P, TILES, P], F32)
                 for i in range(TILES):
-                    nc.tensor.transpose(y_t[:, i, :], y[:, i, t:D:PACK], identity[:])
+                    nc.tensor.transpose(x2_t[:, i, :], x2_all[:, c, i * D + t : (i + 1) * D : PACK], identity[:])
                 nc.scalar.activation(
-                    out=y_t_of_batch[batch][:, t, half * CHUNK : (half + 1) * CHUNK],
-                    in_=y_t[:].rearrange("p i w -> p (i w)"),
+                    out=x2_t_of_batch[batch][:, t, half * CHUNK : (half + 1) * CHUNK],
+                    in_=x2_t[:].rearrange("p i w -> p (i w)"),
                     func=ACT.Identity,
                     accum_out=sums_of_batch[batch][:, 0, t, half : half + 1],
                 )
                 squares = work.tile([P, CHUNK], BF16, bufs=4)
                 nc.scalar.activation(
                     out=squares[:],
-                    in_=y_t[:].rearrange("p i w -> p (i w)"),
+                    in_=x2_t[:].rearrange("p i w -> p (i w)"),
                     func=ACT.Square,
                     accum_out=sums_of_batch[batch][:, 1, t, half : half + 1],
                 )
@@ -204,11 +205,11 @@ def tile_attentionblock_pc_t_kernel(
             gain, shift = norm_of_batch[batch]
             xn_planes = work.tile([P, PACK, CHUNK], BF16)
             for t in range(PACK):
-                y_t_plane = y_t_of_batch[batch][:, t, half * CHUNK : (half + 1) * CHUNK]
+                x2_t_plane = x2_t_of_batch[batch][:, t, half * CHUNK : (half + 1) * CHUNK]
                 if t < PACK // 2:
                     nc.scalar.activation(
                         out=xn_planes[:, t, :],
-                        in_=y_t_plane,
+                        in_=x2_t_plane,
                         func=ACT.Identity,
                         scale=gain[:, t : t + 1],
                         bias=shift[:, t : t + 1],
@@ -216,7 +217,7 @@ def tile_attentionblock_pc_t_kernel(
                 else:
                     nc.vector.tensor_scalar(
                         out=xn_planes[:, t, :],
-                        in0=y_t_plane,
+                        in0=x2_t_plane,
                         scalar1=gain[:, t : t + 1],
                         scalar2=shift[:, t : t + 1],
                         op0=ALU.mult,
@@ -227,7 +228,7 @@ def tile_attentionblock_pc_t_kernel(
             return xn_grouped
 
         def expand(c):
-            ffh = work.tile([P, TILES, D], F32, bufs=3)
+            ffh = work.tile([P, TILES, D], F32)
             for i in range(TILES):
                 product = product_of(xn_mx[c], i, w1_words, w1_plane)
                 nc.vector.tensor_tensor(out=ffh[:, i, :], in0=product[:], in1=b1_rows[:], op=ALU.add)
@@ -247,6 +248,6 @@ def tile_attentionblock_pc_t_kernel(
                 xn_grouped = normalise(step - NORM_LAG)
                 xn_mx[step - NORM_LAG] = quantise(xn_grouped[:].rearrange("p w t -> p (w t)"), "xn")
             if step in chunks:
-                transpose_y(step)
+                transpose_x2(step)
             if step - NORM_LAG - 1 in chunks:
                 expand(step - NORM_LAG - 1)

@@ -23,6 +23,7 @@ CHUNK = TILES * P
 HALVES = TOKENS // CHUNK
 N_CHUNKS = BATCH * HALVES
 NORM_LAG = HALVES
+RUN = 4
 EPS = 1e-5
 
 
@@ -53,7 +54,7 @@ def tile_attentionblock_pc_t_kernel(
         tc.tile_pool(name="work", bufs=2) as work,
         tc.psum_pool(name="attn_t", bufs=2) as attn_t_pool,
         tc.psum_pool(name="product", bufs=3) as product_pool,
-        tc.psum_pool(name="x2_t", bufs=3) as x2_t_pool,
+        tc.psum_pool(name="y_t", bufs=3) as y_t_pool,
     ):
         attn_all = keep.tile([P, N_CHUNKS, TILES * D], BF16)
         x_all = keep.tile([P, N_CHUNKS, TILES * D], BF16)
@@ -72,31 +73,37 @@ def tile_attentionblock_pc_t_kernel(
             load_chunk(attn_rows, attn_all, c)
             load_chunk(x_rows, x_all, c)
 
-        identity = keep.tile([P, P], F32)
-        make_identity(nc, identity[:])
+        one = keep.tile([P, 1], F32)
+        nc.vector.memset(one[:], 1.0)
+        nc.scalar.sqrt(out=one[:], in_=one[:])
 
-        b_merge_rows = keep.tile([P, D], BF16)
-        nc.scalar.dma_start(out=b_merge_rows[:], in_=b_merge.partition_broadcast(P))
-        x2_all = keep.tile([P, N_CHUNKS, TILES * D], F32)
-        for c in range(N_CHUNKS):
-            adder = nc.gpsimd if c < N_CHUNKS // 2 else nc.vector
-            for i in range(TILES):
-                features = slice(i * D, (i + 1) * D)
-                adder.tensor_tensor(out=x2_all[:, c, features], in0=x_all[:, c, features], in1=b_merge_rows[:], op=ALU.add)
-        b1_rows = keep.tile([P, D], BF16)
-        nc.scalar.dma_start(out=b1_rows[:], in_=b1.partition_broadcast(P))
+        ones = keep.tile([P, P], BF16)
+        nc.vector.memset(ones[:], 1.0)
+
+        def spread_over_partitions(bias, label):
+            padded = keep.tile([P, D], BF16, name=label + "_padded")
+            nc.vector.memset(padded[:], 0.0)
+            nc.scalar.dma_start(out=padded[0:1, :], in_=bias.unsqueeze(0))
+            summed = product_pool.tile([P, D], F32, name="product")
+            nc.tensor.matmul(out=summed[:], lhsT=ones[:], rhs=padded[:], start=True, stop=True)
+            rows = keep.tile([P, D], F32, name=label + "_rows")
+            nc.scalar.copy(out=rows[:], in_=summed[:])
+            return rows
+
+        b_merge_rows = spread_over_partitions(b_merge, "b_merge")
+        b1_rows = spread_over_partitions(b1, "b1")
         gamma_pt = keep.tile([P, PACK], BF16)
         nc.scalar.dma_start(out=gamma_pt[:], in_=gamma2.rearrange("a b (p t) -> (a b p) t", t=PACK))
         beta_pt = keep.tile([P, PACK], BF16)
         nc.scalar.dma_start(out=beta_pt[:], in_=beta2.rearrange("a b (p t) -> (a b p) t", t=PACK))
 
-        one = keep.tile([P, 1], F32)
-        nc.vector.memset(one[:], 1.0)
-        nc.scalar.sqrt(out=one[:], in_=one[:])
+        identity = keep.tile([P, P], F32)
+        make_identity(nc, identity[:])
 
         attn_mx = {}
         xn_mx = {}
-        x2_t_of_batch = {}
+        y_of_chunk = {}
+        y_t_of_batch = {}
         sums_of_batch = {}
         norm_of_batch = {}
 
@@ -143,33 +150,37 @@ def tile_attentionblock_pc_t_kernel(
             return product
 
         def merge(c):
+            y = work.tile([P, TILES, D], F32, bufs=3)
+            y_of_chunk[c] = y
+            x2 = work.tile([P, TILES, D], F32, bufs=3)
             for i in range(TILES):
-                features = slice(i * D, (i + 1) * D)
                 product = product_of(attn_mx[c], i, merge_words, merge_plane)
-                nc.vector.tensor_tensor(out=x2_all[:, c, features], in0=product[:], in1=x2_all[:, c, features], op=ALU.add)
-            nc.sync.dma_start(out=x2_rows[c // HALVES][:, chunk_columns(c)], in_=x2_all[:, c, :])
+                nc.vector.tensor_tensor(out=y[:, i, :], in0=product[:], in1=x_all[:, c, i * D : (i + 1) * D], op=ALU.add)
+                nc.vector.tensor_tensor(out=x2[:, i, :], in0=y[:, i, :], in1=b_merge_rows[:], op=ALU.add)
+            nc.sync.dma_start(out=x2_rows[c // HALVES][:, chunk_columns(c)], in_=x2[:].rearrange("p i n -> p (i n)"))
 
-        def transpose_x2(c):
+        def transpose_y(c):
             batch, half = divmod(c, HALVES)
             if half == 0:
-                x2_t_all = work.tile([P, PACK, TOKENS], F32)
-                x2_t_of_batch[batch] = x2_t_all
+                y_t_all = work.tile([P, PACK, TOKENS], F32)
+                y_t_of_batch[batch] = y_t_all
                 sums = work.tile([P, 2, PACK, HALVES], F32)
                 sums_of_batch[batch] = sums
+            y = y_of_chunk[c]
             for t in range(PACK):
-                x2_t = x2_t_pool.tile([P, TILES, P], F32)
+                y_t = y_t_pool.tile([P, TILES, P], F32)
                 for i in range(TILES):
-                    nc.tensor.transpose(x2_t[:, i, :], x2_all[:, c, i * D + t : (i + 1) * D : PACK], identity[:])
+                    nc.tensor.transpose(y_t[:, i, :], y[:, i, t:D:PACK], identity[:])
                 nc.scalar.activation(
-                    out=x2_t_of_batch[batch][:, t, half * CHUNK : (half + 1) * CHUNK],
-                    in_=x2_t[:].rearrange("p i w -> p (i w)"),
+                    out=y_t_of_batch[batch][:, t, half * CHUNK : (half + 1) * CHUNK],
+                    in_=y_t[:].rearrange("p i w -> p (i w)"),
                     func=ACT.Identity,
                     accum_out=sums_of_batch[batch][:, 0, t, half : half + 1],
                 )
                 squares = work.tile([P, CHUNK], BF16, bufs=4)
                 nc.scalar.activation(
                     out=squares[:],
-                    in_=x2_t[:].rearrange("p i w -> p (i w)"),
+                    in_=y_t[:].rearrange("p i w -> p (i w)"),
                     func=ACT.Square,
                     accum_out=sums_of_batch[batch][:, 1, t, half : half + 1],
                 )
@@ -205,34 +216,32 @@ def tile_attentionblock_pc_t_kernel(
             gain, shift = norm_of_batch[batch]
             xn_planes = work.tile([P, PACK, CHUNK], BF16)
             for t in range(PACK):
-                x2_t_plane = x2_t_of_batch[batch][:, t, half * CHUNK : (half + 1) * CHUNK]
-                if t < PACK // 2:
-                    nc.scalar.activation(
-                        out=xn_planes[:, t, :],
-                        in_=x2_t_plane,
-                        func=ACT.Identity,
-                        scale=gain[:, t : t + 1],
-                        bias=shift[:, t : t + 1],
-                    )
-                else:
-                    nc.vector.tensor_scalar(
-                        out=xn_planes[:, t, :],
-                        in0=x2_t_plane,
-                        scalar1=gain[:, t : t + 1],
-                        scalar2=shift[:, t : t + 1],
-                        op0=ALU.mult,
-                        op1=ALU.add,
-                    )
+                y_t_plane = y_t_of_batch[batch][:, t, half * CHUNK : (half + 1) * CHUNK]
+                nc.scalar.activation(
+                    out=xn_planes[:, t, :],
+                    in_=y_t_plane,
+                    func=ACT.Identity,
+                    scale=gain[:, t : t + 1],
+                    bias=shift[:, t : t + 1],
+                )
             xn_grouped = work.tile([P, CHUNK, PACK], BF16, align_bytes=64)
-            nc.vector.tensor_copy(out=xn_grouped[:], in_=xn_planes[:].rearrange("p t w -> p w t"))
+            nc.vector.tensor_copy(
+                out=xn_grouped[:].rearrange("p (c i) t -> p c t i", i=RUN),
+                in_=xn_planes[:].rearrange("p t (c i) -> p c t i", i=RUN),
+            )
             return xn_grouped
 
         def expand(c):
-            ffh = work.tile([P, TILES, D], F32)
+            ffh = work.tile([P, TILES, D], F32, bufs=3)
             for i in range(TILES):
                 product = product_of(xn_mx[c], i, w1_words, w1_plane)
                 nc.vector.tensor_tensor(out=ffh[:, i, :], in0=product[:], in1=b1_rows[:], op=ALU.add)
-            nc.sync.dma_start(out=ffh_rows[c // HALVES][:, chunk_columns(c)], in_=ffh[:].rearrange("p i n -> p (i n)"))
+                if i % 2 == 1:
+                    first = ((c % HALVES) * TILES + i - 1) * D
+                    nc.sync.dma_start(
+                        out=ffh_rows[c // HALVES][:, first : first + 2 * D],
+                        in_=ffh[:, i - 1 : i + 1, :].rearrange("p i n -> p (i n)"),
+                    )
 
         chunks = range(N_CHUNKS)
         for step in range(-1, N_CHUNKS + NORM_LAG + 1):
@@ -248,6 +257,6 @@ def tile_attentionblock_pc_t_kernel(
                 xn_grouped = normalise(step - NORM_LAG)
                 xn_mx[step - NORM_LAG] = quantise(xn_grouped[:].rearrange("p w t -> p (w t)"), "xn")
             if step in chunks:
-                transpose_x2(step)
+                transpose_y(step)
             if step - NORM_LAG - 1 in chunks:
                 expand(step - NORM_LAG - 1)

@@ -66,10 +66,11 @@ def tile_attentionblock_pc_t_kernel(
         load_chunk(attn_rows, attn_all, 0)
         merge_words, merge_plane = load_weight(nc, keep, W_merge_words, W_merge_scales, "merge")
         load_chunk(x_rows, x_all, 0)
-        load_chunk(attn_rows, attn_all, 1)
-        load_chunk(x_rows, x_all, 1)
+        for c in range(1, NORM_LAG + 1):
+            load_chunk(attn_rows, attn_all, c)
+            load_chunk(x_rows, x_all, c)
         w1_words, w1_plane = load_weight(nc, keep, W1_words, W1_scales, "w1")
-        for c in range(2, N_CHUNKS):
+        for c in range(NORM_LAG + 1, N_CHUNKS):
             load_chunk(attn_rows, attn_all, c)
             load_chunk(x_rows, x_all, c)
 
@@ -156,6 +157,7 @@ def tile_attentionblock_pc_t_kernel(
             for i in range(TILES):
                 product = product_of(attn_mx[c], i, merge_words, merge_plane)
                 nc.vector.tensor_tensor(out=y[:, i, :], in0=product[:], in1=x_all[:, c, i * D : (i + 1) * D], op=ALU.add)
+            for i in range(TILES):
                 nc.vector.tensor_tensor(out=x2[:, i, :], in0=y[:, i, :], in1=b_merge_rows[:], op=ALU.add)
             nc.sync.dma_start(out=x2_rows[c // HALVES][:, chunk_columns(c)], in_=x2[:].rearrange("p i n -> p (i n)"))
 
@@ -245,18 +247,20 @@ def tile_attentionblock_pc_t_kernel(
 
         chunks = range(N_CHUNKS)
         for step in range(-1, N_CHUNKS + NORM_LAG + 1):
-            if step - NORM_LAG in chunks and (step - NORM_LAG) % HALVES == 0:
-                norm_coefficients((step - NORM_LAG) // HALVES)
-            if step + 1 in chunks:
-                attn_grouped = transpose_attn(step + 1)
+            ahead, normed, expanded = step + 1, step - NORM_LAG, step - NORM_LAG - 1
+            if normed in chunks and normed % HALVES == 0:
+                norm_coefficients(normed // HALVES)
+            if ahead in chunks:
+                attn_grouped = transpose_attn(ahead)
+            if normed in chunks:
+                xn_grouped = normalise(normed)
             if step in chunks:
                 merge(step)
-            if step + 1 in chunks:
-                attn_mx[step + 1] = quantise(attn_grouped[:], "attn")
-            if step - NORM_LAG in chunks:
-                xn_grouped = normalise(step - NORM_LAG)
-                xn_mx[step - NORM_LAG] = quantise(xn_grouped[:].rearrange("p w t -> p (w t)"), "xn")
+            if ahead in chunks:
+                attn_mx[ahead] = quantise(attn_grouped[:], "attn")
+            if normed in chunks:
+                xn_mx[normed] = quantise(xn_grouped[:].rearrange("p w t -> p (w t)"), "xn")
             if step in chunks:
                 transpose_y(step)
-            if step - NORM_LAG - 1 in chunks:
-                expand(step - NORM_LAG - 1)
+            if expanded in chunks:
+                expand(expanded)

@@ -24,6 +24,7 @@ HALVES = TOKENS // CHUNK
 N_CHUNKS = BATCH * HALVES
 NORM_LAG = HALVES
 RUN = 4
+SCALAR_SLABS = 0
 EPS = 1e-5
 
 
@@ -52,9 +53,9 @@ def tile_attentionblock_pc_t_kernel(
     with (
         tc.tile_pool(name="keep", bufs=1) as keep,
         tc.tile_pool(name="work", bufs=2) as work,
-        tc.psum_pool(name="attn_t", bufs=2) as attn_t_pool,
+        tc.psum_pool(name="turned", bufs=2) as turned_pool,
         tc.psum_pool(name="product", bufs=3) as product_pool,
-        tc.psum_pool(name="y_t", bufs=3) as y_t_pool,
+        tc.psum_pool(name="x2_back", bufs=3) as x2_back_pool,
     ):
         attn_all = keep.tile([P, N_CHUNKS, TILES * D], BF16)
         x_all = keep.tile([P, N_CHUNKS, TILES * D], BF16)
@@ -64,7 +65,7 @@ def tile_attentionblock_pc_t_kernel(
             nc.sync.dma_start(out=resident[:, c, :], in_=rows[batch][:, half * TILES * D : (half + 1) * TILES * D])
 
         load_chunk(attn_rows, attn_all, 0)
-        merge_words, merge_plane = load_weight(nc, keep, W_merge_words, W_merge_scales, "merge")
+        merge_words_given, merge_plane_given = load_weight(nc, keep, W_merge_words, W_merge_scales, "merge_given")
         load_chunk(x_rows, x_all, 0)
         for c in range(1, NORM_LAG + 1):
             load_chunk(attn_rows, attn_all, c)
@@ -74,25 +75,32 @@ def tile_attentionblock_pc_t_kernel(
             load_chunk(attn_rows, attn_all, c)
             load_chunk(x_rows, x_all, c)
 
+        merge_words = keep.tile([P, D], U32, align_bytes=64)
+        nc.vector.tensor_copy(
+            out=merge_words[:].bitcast(I32).rearrange("p (t m) -> p t m", t=PACK),
+            in_=merge_words_given[:].bitcast(I32).rearrange("p (m t) -> p t m", t=PACK),
+        )
+        merge_plane = keep.tile([P, D], U8, align_bytes=64)
+        nc.vector.tensor_copy(
+            out=merge_plane[:].rearrange("p (t m) -> p m t", t=PACK),
+            in_=merge_plane_given[:].rearrange("p (m t) -> p m t", t=PACK),
+        )
+
         one = keep.tile([P, 1], F32)
         nc.vector.memset(one[:], 1.0)
         nc.scalar.sqrt(out=one[:], in_=one[:])
 
         ones = keep.tile([P, P], BF16)
         nc.vector.memset(ones[:], 1.0)
-
-        def spread_over_partitions(bias, label):
-            padded = keep.tile([P, D], BF16, name=label + "_padded")
-            nc.vector.memset(padded[:], 0.0)
-            nc.scalar.dma_start(out=padded[0:1, :], in_=bias.unsqueeze(0))
-            summed = product_pool.tile([P, D], F32, name="product")
-            nc.tensor.matmul(out=summed[:], lhsT=ones[:], rhs=padded[:], start=True, stop=True)
-            rows = keep.tile([P, D], F32, name=label + "_rows")
-            nc.scalar.copy(out=rows[:], in_=summed[:])
-            return rows
-
-        b_merge_rows = spread_over_partitions(b_merge, "b_merge")
-        b1_rows = spread_over_partitions(b1, "b1")
+        b1_padded = keep.tile([P, D], BF16)
+        nc.vector.memset(b1_padded[:], 0.0)
+        nc.scalar.dma_start(out=b1_padded[0:1, :], in_=b1.unsqueeze(0))
+        b1_summed = product_pool.tile([P, D], F32, name="product")
+        nc.tensor.matmul(out=b1_summed[:], lhsT=ones[:], rhs=b1_padded[:], start=True, stop=True)
+        b1_rows = keep.tile([P, D], F32)
+        nc.scalar.copy(out=b1_rows[:], in_=b1_summed[:])
+        b_merge_pt = keep.tile([P, PACK], BF16)
+        nc.scalar.dma_start(out=b_merge_pt[:], in_=b_merge.rearrange("(p t) -> p t", t=PACK))
         gamma_pt = keep.tile([P, PACK], BF16)
         nc.scalar.dma_start(out=gamma_pt[:], in_=gamma2.rearrange("a b (p t) -> (a b p) t", t=PACK))
         beta_pt = keep.tile([P, PACK], BF16)
@@ -103,8 +111,8 @@ def tile_attentionblock_pc_t_kernel(
 
         attn_mx = {}
         xn_mx = {}
-        y_of_chunk = {}
-        y_t_of_batch = {}
+        x_turned = {}
+        x2_t_of_batch = {}
         sums_of_batch = {}
         norm_of_batch = {}
 
@@ -112,22 +120,20 @@ def tile_attentionblock_pc_t_kernel(
             half = c % HALVES
             return slice(half * TILES * D, (half + 1) * TILES * D)
 
-        def transpose_attn(c):
-            attn_words = attn_all[:, c, :].bitcast(F32)
-            attn_grouped = work.tile([P, CHUNK * PACK], BF16, align_bytes=64)
-            grouped_words = attn_grouped[:].bitcast(F32).rearrange("p (i w u) -> p i w u", i=TILES, u=2)
-            for pair in range(TILES // 2):
-                attn_t = attn_t_pool.tile([P, 2, 2, P], F32)
+        def turn(resident, c, label):
+            pairs = resident[:, c, :].bitcast(F32)
+            grouped = work.tile([P, CHUNK * PACK], BF16, name=label + "_grouped", align_bytes=64)
+            grouped_pairs = grouped[:].bitcast(F32).rearrange("p (i w u) -> p i w u", i=TILES, u=2)
+            for two in range(TILES // 2):
+                turned = turned_pool.tile([P, 2, 2, P], F32)
                 for j in range(2):
-                    first_word = (2 * pair + j) * (D // 2)
+                    first = (2 * two + j) * (D // 2)
                     for u in range(2):
-                        nc.tensor.transpose(
-                            attn_t[:, j, u, :], attn_words[:, first_word + u : first_word + D // 2 : 2], identity[:]
-                        )
+                        nc.tensor.transpose(turned[:, j, u, :], pairs[:, first + u : first + D // 2 : 2], identity[:])
                 nc.scalar.copy(
-                    out=grouped_words[:, 2 * pair : 2 * pair + 2], in_=attn_t[:].rearrange("p j u w -> p j w u")
+                    out=grouped_pairs[:, 2 * two : 2 * two + 2], in_=turned[:].rearrange("p j u w -> p j w u")
                 )
-            return attn_grouped
+            return grouped
 
         def quantise(grouped, label):
             codes = work.tile([P, CHUNK], U32, name=label + "_codes", align_bytes=64)
@@ -135,57 +141,60 @@ def tile_attentionblock_pc_t_kernel(
             nc.vector.quantize_mx(out=codes[:].bitcast(FP8X4), scales=plane[:], in_=grouped)
             return codes, plane
 
-        def product_of(activation_mx, i, weight_words, weight_plane):
-            codes, plane = activation_mx
-            tokens = slice(i * P, (i + 1) * P)
-            product = product_pool.tile([P, D], F32)
-            nc.tensor.matmul_mx(
-                out=product[:],
-                lhsT=codes[:, tokens].bitcast(FP8X4),
-                lhsT_scale=plane[:, tokens],
-                rhs=weight_words[:].bitcast(FP8X4),
-                rhs_scale=weight_plane[:],
-                start=True,
-                stop=True,
-            )
-            return product
-
         def merge(c):
-            y = work.tile([P, TILES, D], F32, bufs=3)
-            y_of_chunk[c] = y
-            x2 = work.tile([P, TILES, D], F32, bufs=3)
-            for i in range(TILES):
-                product = product_of(attn_mx[c], i, merge_words, merge_plane)
-                nc.vector.tensor_tensor(out=y[:, i, :], in0=product[:], in1=x_all[:, c, i * D : (i + 1) * D], op=ALU.add)
-            for i in range(TILES):
-                nc.vector.tensor_tensor(out=x2[:, i, :], in0=y[:, i, :], in1=b_merge_rows[:], op=ALU.add)
-            nc.sync.dma_start(out=x2_rows[c // HALVES][:, chunk_columns(c)], in_=x2[:].rearrange("p i n -> p (i n)"))
-
-        def transpose_y(c):
             batch, half = divmod(c, HALVES)
             if half == 0:
-                y_t_all = work.tile([P, PACK, TOKENS], F32)
-                y_t_of_batch[batch] = y_t_all
+                x2_t_all = work.tile([P, PACK, TOKENS], F32)
+                x2_t_of_batch[batch] = x2_t_all
                 sums = work.tile([P, 2, PACK, HALVES], F32)
                 sums_of_batch[batch] = sums
-            y = y_of_chunk[c]
+            codes, plane = attn_mx[c]
+            x_by_slab = x_turned[c][:].rearrange("p (w t) -> p t w", t=PACK)
             for t in range(PACK):
-                y_t = y_t_pool.tile([P, TILES, P], F32)
-                for i in range(TILES):
-                    nc.tensor.transpose(y_t[:, i, :], y[:, i, t:D:PACK], identity[:])
-                nc.scalar.activation(
-                    out=y_t_of_batch[batch][:, t, half * CHUNK : (half + 1) * CHUNK],
-                    in_=y_t[:].rearrange("p i w -> p (i w)"),
-                    func=ACT.Identity,
+                slab = slice(t * P, (t + 1) * P)
+                product = product_pool.tile([P, CHUNK], F32)
+                nc.tensor.matmul_mx(
+                    out=product[:],
+                    lhsT=merge_words[:, slab].bitcast(FP8X4),
+                    lhsT_scale=merge_plane[:, slab],
+                    rhs=codes[:].bitcast(FP8X4),
+                    rhs_scale=plane[:],
+                    start=True,
+                    stop=True,
+                )
+                nc.vector.scalar_tensor_tensor(
+                    out=x2_t_of_batch[batch][:, t, half * CHUNK : (half + 1) * CHUNK],
+                    in0=product[:],
+                    scalar=b_merge_pt[:, t : t + 1],
+                    in1=x_by_slab[:, t, :],
+                    op0=ALU.add,
+                    op1=ALU.add,
                     accum_out=sums_of_batch[batch][:, 0, t, half : half + 1],
                 )
+
+        def square_sums(c):
+            batch, half = divmod(c, HALVES)
+            for t in range(PACK):
                 squares = work.tile([P, CHUNK], BF16, bufs=4)
                 nc.scalar.activation(
                     out=squares[:],
-                    in_=y_t[:].rearrange("p i w -> p (i w)"),
+                    in_=x2_t_of_batch[batch][:, t, half * CHUNK : (half + 1) * CHUNK],
                     func=ACT.Square,
                     accum_out=sums_of_batch[batch][:, 1, t, half : half + 1],
                 )
+
+        def turn_back(c):
+            batch, half = divmod(c, HALVES)
+            x2 = work.tile([P, TILES, D], F32, bufs=3)
+            for i in range(TILES):
+                x2_back = x2_back_pool.tile([P, PACK, P], F32)
+                first = half * CHUNK + i * P
+                for t in range(PACK):
+                    nc.tensor.transpose(x2_back[:, t, :], x2_t_of_batch[batch][:, t, first : first + P], identity[:])
+                nc.scalar.copy(
+                    out=x2[:, i, :].rearrange("p (m t) -> p m t", t=PACK), in_=x2_back[:].rearrange("p t m -> p m t")
+                )
+            nc.sync.dma_start(out=x2_rows[batch][:, chunk_columns(c)], in_=x2[:].rearrange("p i n -> p (i n)"))
 
         def norm_coefficients(batch):
             totals = work.tile([P, 2 * PACK], F32)
@@ -216,27 +225,48 @@ def tile_attentionblock_pc_t_kernel(
         def normalise(c):
             batch, half = divmod(c, HALVES)
             gain, shift = norm_of_batch[batch]
-            xn_planes = work.tile([P, PACK, CHUNK], BF16)
+            xn_slabs = work.tile([P, PACK, CHUNK], BF16)
             for t in range(PACK):
-                y_t_plane = y_t_of_batch[batch][:, t, half * CHUNK : (half + 1) * CHUNK]
-                nc.scalar.activation(
-                    out=xn_planes[:, t, :],
-                    in_=y_t_plane,
-                    func=ACT.Identity,
-                    scale=gain[:, t : t + 1],
-                    bias=shift[:, t : t + 1],
-                )
+                x2_t_slab = x2_t_of_batch[batch][:, t, half * CHUNK : (half + 1) * CHUNK]
+                if t < SCALAR_SLABS:
+                    nc.scalar.activation(
+                        out=xn_slabs[:, t, :],
+                        in_=x2_t_slab,
+                        func=ACT.Identity,
+                        scale=gain[:, t : t + 1],
+                        bias=shift[:, t : t + 1],
+                    )
+                else:
+                    nc.vector.tensor_scalar(
+                        out=xn_slabs[:, t, :],
+                        in0=x2_t_slab,
+                        scalar1=gain[:, t : t + 1],
+                        scalar2=shift[:, t : t + 1],
+                        op0=ALU.mult,
+                        op1=ALU.add,
+                    )
             xn_grouped = work.tile([P, CHUNK, PACK], BF16, align_bytes=64)
             nc.vector.tensor_copy(
                 out=xn_grouped[:].rearrange("p (c i) t -> p c t i", i=RUN),
-                in_=xn_planes[:].rearrange("p t (c i) -> p c t i", i=RUN),
+                in_=xn_slabs[:].rearrange("p t (c i) -> p c t i", i=RUN),
             )
             return xn_grouped
 
         def expand(c):
+            codes, plane = xn_mx[c]
             ffh = work.tile([P, TILES, D], F32, bufs=3)
             for i in range(TILES):
-                product = product_of(xn_mx[c], i, w1_words, w1_plane)
+                tokens = slice(i * P, (i + 1) * P)
+                product = product_pool.tile([P, D], F32)
+                nc.tensor.matmul_mx(
+                    out=product[:],
+                    lhsT=codes[:, tokens].bitcast(FP8X4),
+                    lhsT_scale=plane[:, tokens],
+                    rhs=w1_words[:].bitcast(FP8X4),
+                    rhs_scale=w1_plane[:],
+                    start=True,
+                    stop=True,
+                )
                 nc.vector.tensor_tensor(out=ffh[:, i, :], in0=product[:], in1=b1_rows[:], op=ALU.add)
                 if i % 2 == 1:
                     first = ((c % HALVES) * TILES + i - 1) * D
@@ -251,7 +281,8 @@ def tile_attentionblock_pc_t_kernel(
             if normed in chunks and normed % HALVES == 0:
                 norm_coefficients(normed // HALVES)
             if ahead in chunks:
-                attn_grouped = transpose_attn(ahead)
+                attn_grouped = turn(attn_all, ahead, "attn")
+                x_turned[ahead] = turn(x_all, ahead, "x")
             if normed in chunks:
                 xn_grouped = normalise(normed)
             if step in chunks:
@@ -261,6 +292,7 @@ def tile_attentionblock_pc_t_kernel(
             if normed in chunks:
                 xn_mx[normed] = quantise(xn_grouped[:].rearrange("p w t -> p (w t)"), "xn")
             if step in chunks:
-                transpose_y(step)
+                turn_back(step)
+                square_sums(step)
             if expanded in chunks:
                 expand(expanded)

@@ -124,7 +124,8 @@ def tile_attentionblock_pc_t_kernel(
             pairs = resident[:, c, :].bitcast(F32)
             grouped = work.tile([P, CHUNK * PACK], BF16, name=label + "_grouped", align_bytes=64)
             grouped_pairs = grouped[:].bitcast(F32).rearrange("p (i w u) -> p i w u", i=TILES, u=2)
-            for two in range(TILES // 2):
+
+            def turn_two(two):
                 turned = turned_pool.tile([P, 2, 2, P], F32)
                 for j in range(2):
                     first = (2 * two + j) * (D // 2)
@@ -133,7 +134,8 @@ def tile_attentionblock_pc_t_kernel(
                 nc.scalar.copy(
                     out=grouped_pairs[:, 2 * two : 2 * two + 2], in_=turned[:].rearrange("p j u w -> p j w u")
                 )
-            return grouped
+
+            return grouped, turn_two
 
         def quantise(grouped, label):
             codes = work.tile([P, CHUNK], U32, name=label + "_codes", align_bytes=64)
@@ -150,7 +152,8 @@ def tile_attentionblock_pc_t_kernel(
                 sums_of_batch[batch] = sums
             codes, plane = attn_mx[c]
             x_by_slab = x_turned[c][:].rearrange("p (w t) -> p t w", t=PACK)
-            for t in range(PACK):
+
+            def merge_slab(t):
                 slab = slice(t * P, (t + 1) * P)
                 product = product_pool.tile([P, CHUNK], F32)
                 nc.tensor.matmul_mx(
@@ -172,6 +175,8 @@ def tile_attentionblock_pc_t_kernel(
                     accum_out=sums_of_batch[batch][:, 0, t, half : half + 1],
                 )
 
+            return merge_slab
+
         def square_sums(c):
             batch, half = divmod(c, HALVES)
             for t in range(PACK):
@@ -186,7 +191,8 @@ def tile_attentionblock_pc_t_kernel(
         def turn_back(c):
             batch, half = divmod(c, HALVES)
             x2 = work.tile([P, TILES, D], F32, bufs=3)
-            for i in range(TILES):
+
+            def turn_back_tile(i):
                 x2_back = x2_back_pool.tile([P, PACK, P], F32)
                 first = half * CHUNK + i * P
                 for t in range(PACK):
@@ -194,7 +200,10 @@ def tile_attentionblock_pc_t_kernel(
                 nc.scalar.copy(
                     out=x2[:, i, :].rearrange("p (m t) -> p m t", t=PACK), in_=x2_back[:].rearrange("p t m -> p m t")
                 )
-            nc.sync.dma_start(out=x2_rows[batch][:, chunk_columns(c)], in_=x2[:].rearrange("p i n -> p (i n)"))
+                if i == TILES - 1:
+                    nc.sync.dma_start(out=x2_rows[batch][:, chunk_columns(c)], in_=x2[:].rearrange("p i n -> p (i n)"))
+
+            return turn_back_tile
 
         def norm_coefficients(batch):
             totals = work.tile([P, 2 * PACK], F32)
@@ -255,7 +264,8 @@ def tile_attentionblock_pc_t_kernel(
         def expand(c):
             codes, plane = xn_mx[c]
             ffh = work.tile([P, TILES, D], F32, bufs=3)
-            for i in range(TILES):
+
+            def expand_tile(i):
                 tokens = slice(i * P, (i + 1) * P)
                 product = product_pool.tile([P, D], F32)
                 nc.tensor.matmul_mx(
@@ -275,24 +285,47 @@ def tile_attentionblock_pc_t_kernel(
                         in_=ffh[:, i - 1 : i + 1, :].rearrange("p i n -> p (i n)"),
                     )
 
+            return expand_tile
+
         chunks = range(N_CHUNKS)
-        for step in range(-1, N_CHUNKS + NORM_LAG + 1):
-            ahead, normed, expanded = step + 1, step - NORM_LAG, step - NORM_LAG - 1
-            if normed in chunks and normed % HALVES == 0:
-                norm_coefficients(normed // HALVES)
-            if ahead in chunks:
-                attn_grouped = turn(attn_all, ahead, "attn")
-                x_turned[ahead] = turn(x_all, ahead, "x")
-            if normed in chunks:
-                xn_grouped = normalise(normed)
-            if step in chunks:
-                merge(step)
-            if ahead in chunks:
-                attn_mx[ahead] = quantise(attn_grouped[:], "attn")
-            if normed in chunks:
-                xn_mx[normed] = quantise(xn_grouped[:].rearrange("p w t -> p (w t)"), "xn")
-            if step in chunks:
-                turn_back(step)
-                square_sums(step)
-            if expanded in chunks:
-                expand(expanded)
+        with tc.manual_schedule(engines={mybir.EngineType.PE}):
+            for step in range(-1, N_CHUNKS + NORM_LAG + 1):
+                ahead, back, normed, expanded = step + 1, step - 1, step - NORM_LAG, step - NORM_LAG - 1
+                if normed in chunks and normed % HALVES == 0:
+                    norm_coefficients(normed // HALVES)
+                if step in chunks:
+                    merge_slab = merge(step)
+                    merge_slab(0)
+                    merge_slab(1)
+                if ahead in chunks:
+                    attn_grouped, turn_two = turn(attn_all, ahead, "attn")
+                    turn_two(0)
+                    turn_two(1)
+                if normed in chunks:
+                    xn_grouped = normalise(normed)
+                if step in chunks:
+                    merge_slab(2)
+                    merge_slab(3)
+                if ahead in chunks:
+                    x_turned[ahead], turn_two = turn(x_all, ahead, "x")
+                    turn_two(0)
+                    turn_two(1)
+                    attn_mx[ahead] = quantise(attn_grouped[:], "attn")
+                if expanded in chunks:
+                    expand_tile = expand(expanded)
+                    expand_tile(0)
+                    expand_tile(1)
+                if normed in chunks:
+                    xn_mx[normed] = quantise(xn_grouped[:].rearrange("p w t -> p (w t)"), "xn")
+                if back in chunks:
+                    turn_back_tile = turn_back(back)
+                    turn_back_tile(0)
+                    turn_back_tile(1)
+                if expanded in chunks:
+                    expand_tile(2)
+                    expand_tile(3)
+                if back in chunks:
+                    turn_back_tile(2)
+                    turn_back_tile(3)
+                if step in chunks:
+                    square_sums(step)

@@ -24,7 +24,7 @@ HALVES = TOKENS // CHUNK
 N_CHUNKS = BATCH * HALVES
 NORM_LAG = HALVES
 RUN = 4
-SCALAR_SLABS = 0
+SCALAR_SLABS = 2
 EPS = 1e-5
 
 

@@ -53,9 +53,8 @@ def tile_attentionblock_pc_t_kernel(
     with (
         tc.tile_pool(name="keep", bufs=1) as keep,
         tc.tile_pool(name="work", bufs=2) as work,
-        tc.psum_pool(name="turned", bufs=2) as turned_pool,
+        tc.psum_pool(name="turned", bufs=5) as turned_pool,
         tc.psum_pool(name="product", bufs=3) as product_pool,
-        tc.psum_pool(name="x2_back", bufs=3) as x2_back_pool,
     ):
         attn_all = keep.tile([P, N_CHUNKS, TILES * D], BF16)
         x_all = keep.tile([P, N_CHUNKS, TILES * D], BF16)
@@ -64,9 +63,14 @@ def tile_attentionblock_pc_t_kernel(
             batch, half = divmod(c, HALVES)
             nc.sync.dma_start(out=resident[:, c, :], in_=rows[batch][:, half * TILES * D : (half + 1) * TILES * D])
 
-        load_chunk(attn_rows, attn_all, 0)
+        def load_first_chunk(rows, resident):
+            for part in range(2):
+                columns = slice(part * TILES * D // 2, (part + 1) * TILES * D // 2)
+                nc.sync.dma_start(out=resident[:, 0, columns], in_=rows[0][:, columns])
+
+        load_first_chunk(attn_rows, attn_all)
         merge_words_given, merge_plane_given = load_weight(nc, keep, W_merge_words, W_merge_scales, "merge_given")
-        load_chunk(x_rows, x_all, 0)
+        load_first_chunk(x_rows, x_all)
         for c in range(1, NORM_LAG + 1):
             load_chunk(attn_rows, attn_all, c)
             load_chunk(x_rows, x_all, c)
@@ -193,13 +197,12 @@ def tile_attentionblock_pc_t_kernel(
             x2 = work.tile([P, TILES, D], F32, bufs=3)
 
             def turn_back_tile(i):
-                x2_back = x2_back_pool.tile([P, PACK, P], F32)
+                x2_back = turned_pool.tile([P, PACK, P], F32, name="turned")
                 first = half * CHUNK + i * P
                 for t in range(PACK):
                     nc.tensor.transpose(x2_back[:, t, :], x2_t_of_batch[batch][:, t, first : first + P], identity[:])
-                nc.scalar.copy(
-                    out=x2[:, i, :].rearrange("p (m t) -> p m t", t=PACK), in_=x2_back[:].rearrange("p t m -> p m t")
-                )
+                copier = nc.vector.tensor_copy if batch == 0 and i < TILES // 2 else nc.scalar.copy
+                copier(out=x2[:, i, :].rearrange("p (m t) -> p m t", t=PACK), in_=x2_back[:].rearrange("p t m -> p m t"))
                 if i == TILES - 1:
                     nc.sync.dma_start(out=x2_rows[batch][:, chunk_columns(c)], in_=x2[:].rearrange("p i n -> p (i n)"))
 
@@ -278,11 +281,12 @@ def tile_attentionblock_pc_t_kernel(
                     stop=True,
                 )
                 nc.vector.tensor_tensor(out=ffh[:, i, :], in0=product[:], in1=b1_rows[:], op=ALU.add)
-                if i % 2 == 1:
-                    first = ((c % HALVES) * TILES + i - 1) * D
+                together = 1 if c == N_CHUNKS - 1 else 2
+                if (i + 1) % together == 0:
+                    first = ((c % HALVES) * TILES + i + 1 - together) * D
                     nc.sync.dma_start(
-                        out=ffh_rows[c // HALVES][:, first : first + 2 * D],
-                        in_=ffh[:, i - 1 : i + 1, :].rearrange("p i n -> p (i n)"),
+                        out=ffh_rows[c // HALVES][:, first : first + together * D],
+                        in_=ffh[:, i + 1 - together : i + 1, :].rearrange("p i n -> p (i n)"),
                     )
 
             return expand_tile

@@ -23,7 +23,7 @@ CHUNK = TILES * P
 HALVES = TOKENS // CHUNK
 N_CHUNKS = BATCH * HALVES
 NORM_LAG = HALVES
-RUN = 4
+RUN = 8
 SCALAR_SLABS = 2
 EPS = 1e-5
 

@@ -53,8 +53,8 @@ def tile_attentionblock_pc_t_kernel(
     with (
         tc.tile_pool(name="keep", bufs=1) as keep,
         tc.tile_pool(name="work", bufs=2) as work,
-        tc.psum_pool(name="turned", bufs=5) as turned_pool,
-        tc.psum_pool(name="product", bufs=3) as product_pool,
+        tc.psum_pool(name="turned", bufs=4) as turned_pool,
+        tc.psum_pool(name="product", bufs=4) as product_pool,
     ):
         attn_all = keep.tile([P, N_CHUNKS, TILES * D], BF16)
         x_all = keep.tile([P, N_CHUNKS, TILES * D], BF16)

@@ -118,6 +118,8 @@ def tile_attentionblock_pc_t_kernel(
         x_turned = {}
         x2_t_of_batch = {}
         sums_of_batch = {}
+        squares_of_batch = {}
+        mean_terms_of_batch = {}
         norm_of_batch = {}
 
         def chunk_columns(c):
@@ -152,8 +154,10 @@ def tile_attentionblock_pc_t_kernel(
             if half == 0:
                 x2_t_all = work.tile([P, PACK, TOKENS], F32)
                 x2_t_of_batch[batch] = x2_t_all
-                sums = work.tile([P, 2, PACK, HALVES], F32)
+                sums = work.tile([P, PACK, HALVES], F32)
                 sums_of_batch[batch] = sums
+                square_terms = work.tile([P, PACK, HALVES + 1], F32)
+                squares_of_batch[batch] = square_terms
             codes, plane = attn_mx[c]
             x_by_slab = x_turned[c][:].rearrange("p (w t) -> p t w", t=PACK)
 
@@ -176,7 +180,7 @@ def tile_attentionblock_pc_t_kernel(
                     in1=x_by_slab[:, t, :],
                     op0=ALU.add,
                     op1=ALU.add,
-                    accum_out=sums_of_batch[batch][:, 0, t, half : half + 1],
+                    accum_out=sums_of_batch[batch][:, t, half : half + 1],
                 )
 
             return merge_slab
@@ -189,7 +193,7 @@ def tile_attentionblock_pc_t_kernel(
                     out=squares[:],
                     in_=x2_t_of_batch[batch][:, t, half * CHUNK : (half + 1) * CHUNK],
                     func=ACT.Square,
-                    accum_out=sums_of_batch[batch][:, 1, t, half : half + 1],
+                    accum_out=squares_of_batch[batch][:, t, half : half + 1],
                 )
 
         def turn_back(c):
@@ -208,30 +212,36 @@ def tile_attentionblock_pc_t_kernel(
 
             return turn_back_tile
 
-        def norm_coefficients(batch):
-            totals = work.tile([P, 2 * PACK], F32)
-            nc.vector.tensor_reduce(
-                out=totals[:], in_=sums_of_batch[batch][:].rearrange("p k t h -> p (k t) h"), axis=AXIS.X, op=ALU.add
-            )
-            moments = work.tile([P, 2, PACK], F32)
-            nc.vector.tensor_scalar_mul(moments[:].rearrange("p k t -> p (k t)"), totals[:], 1.0 / TOKENS)
-            mean = moments[:, 0, :]
-            mean_squared = work.tile([P, PACK], F32)
-            nc.vector.tensor_mul(mean_squared[:], mean, mean)
-            var_eps = work.tile([P, PACK], F32)
+        def mean_terms(batch):
+            total = work.tile([P, PACK], F32)
+            nc.vector.tensor_reduce(out=total[:], in_=sums_of_batch[batch][:], axis=AXIS.X, op=ALU.add)
             nc.vector.scalar_tensor_tensor(
-                out=var_eps[:], in0=moments[:, 1, :], scalar=EPS, in1=mean_squared[:], op0=ALU.add, op1=ALU.subtract
+                out=squares_of_batch[batch][:, :, HALVES],
+                in0=total[:],
+                scalar=-1.0 / TOKENS,
+                in1=total[:],
+                op0=ALU.mult,
+                op1=ALU.mult,
             )
+            minus_mean_gamma = work.tile([P, PACK], F32)
+            nc.vector.scalar_tensor_tensor(
+                out=minus_mean_gamma[:], in0=total[:], scalar=-1.0 / TOKENS, in1=gamma_pt[:], op0=ALU.mult, op1=ALU.mult
+            )
+            mean_terms_of_batch[batch] = minus_mean_gamma
+
+        def norm_coefficients(batch):
+            spread = work.tile([P, PACK], F32)
+            nc.vector.tensor_reduce(out=spread[:], in_=squares_of_batch[batch][:], axis=AXIS.X, op=ALU.add)
             std = work.tile([P, PACK], F32)
-            nc.scalar.sqrt(out=std[:], in_=var_eps[:])
+            nc.scalar.activation(out=std[:], in_=spread[:], func=ACT.Sqrt, scale=1.0 / TOKENS, bias=EPS)
             rstd = work.tile([P, PACK], F32)
             nc.vector.reciprocal(rstd[:], std[:])
+            minus_mean_gain = work.tile([P, PACK], F32)
+            nc.vector.tensor_mul(minus_mean_gain[:], mean_terms_of_batch[batch][:], rstd[:])
             gain = work.tile([P, PACK], F32)
             nc.vector.tensor_mul(gain[:], gamma_pt[:], rstd[:])
-            mean_gain = work.tile([P, PACK], F32)
-            nc.vector.tensor_mul(mean_gain[:], mean, gain[:])
             shift = work.tile([P, PACK], F32)
-            nc.vector.tensor_sub(shift[:], beta_pt[:], mean_gain[:])
+            nc.vector.tensor_add(shift[:], minus_mean_gain[:], beta_pt[:])
             norm_of_batch[batch] = (gain, shift)
 
         def normalise(c):
@@ -310,6 +320,9 @@ def tile_attentionblock_pc_t_kernel(
                 if step in chunks:
                     merge_slab(2)
                     merge_slab(3)
+                    square_sums(step)
+                    if step % HALVES == HALVES - 1:
+                        mean_terms(step // HALVES)
                 if ahead in chunks:
                     x_turned[ahead], turn_two = turn(x_all, ahead, "x")
                     turn_two(0)
@@ -331,5 +344,3 @@ def tile_attentionblock_pc_t_kernel(
                 if back in chunks:
                     turn_back_tile(2)
                     turn_back_tile(3)
-                if step in chunks:
-                    square_sums(step)

@@ -320,7 +320,6 @@ def tile_attentionblock_pc_t_kernel(
                 if step in chunks:
                     merge_slab(2)
                     merge_slab(3)
-                    square_sums(step)
                     if step % HALVES == HALVES - 1:
                         mean_terms(step // HALVES)
                 if ahead in chunks:
@@ -344,3 +343,5 @@ def tile_attentionblock_pc_t_kernel(
                 if back in chunks:
                     turn_back_tile(2)
                     turn_back_tile(3)
+                if step in chunks:
+                    square_sums(step)

import concourse.mybir as mybir
from concourse.masks import make_identity

FLOPS = 2 * 2 * 4096 * 512 * 512

FP8X4 = mybir.dt.float8_e4m3fn_x4
BF16 = mybir.dt.bfloat16
F32 = mybir.dt.float32
I32 = mybir.dt.int32
U32 = mybir.dt.uint32
U8 = mybir.dt.uint8
ACT = mybir.ActivationFunctionType
ALU = mybir.AluOpType
AXIS = mybir.AxisListType

P = 128
PACK = 4
D = P * PACK
BATCH = 4
TOKENS = 1024
TILES = 4
CHUNK = TILES * P
HALVES = TOKENS // CHUNK
N_CHUNKS = BATCH * HALVES
NORM_LAG = HALVES
RUN = 8
SCALAR_SLABS = 2
EPS = 1e-5


def load_weight(nc, pool, words_dram, scales_dram, label):
    words = pool.tile([P, D], U32, name=label + "_words", align_bytes=64)
    plane = pool.tile([P, D], U8, name=label + "_plane", align_bytes=64)
    nc.vector.memset(plane[:].bitcast(I32), 0)
    for quadrant in range(4):
        nc.sync.dma_start(
            out=plane[32 * quadrant : 32 * quadrant + 4, :].bitcast(I32),
            in_=scales_dram[0, 4 * quadrant : 4 * quadrant + 4, :].bitcast(I32),
        )
    nc.sync.dma_start(out=words[:].bitcast(I32), in_=words_dram[0].rearrange("p n t -> p (n t)").bitcast(I32))
    return words, plane


def tile_attentionblock_pc_t_kernel(
    tc, attn_out, x, W_merge_words, W_merge_scales, b_merge, gamma2, beta2, W1_words, W1_scales, b1, out_0, out_1
):
    nc = tc.nc
    attn_rows = attn_out.rearrange("b (p i) k -> b p (i k)", p=P)
    x_rows = x.rearrange("b (p i) k -> b p (i k)", p=P)
    x2_rows = out_0.rearrange("b (p i) n -> b p (i n)", p=P)
    ffh_rows = out_1.rearrange("b (p i) n -> b p (i n)", p=P)

    with (
        tc.tile_pool(name="keep", bufs=1) as keep,
        tc.tile_pool(name="work", bufs=2) as work,
        tc.psum_pool(name="turned", bufs=4) as turned_pool,
        tc.psum_pool(name="product", bufs=4) as product_pool,
    ):
        attn_all = keep.tile([P, N_CHUNKS, TILES * D], BF16)
        x_all = keep.tile([P, N_CHUNKS, TILES * D], BF16)

        def load_chunk(rows, resident, c):
            batch, half = divmod(c, HALVES)
            nc.sync.dma_start(out=resident[:, c, :], in_=rows[batch][:, half * TILES * D : (half + 1) * TILES * D])

        def load_first_chunk(rows, resident):
            for part in range(2):
                columns = slice(part * TILES * D // 2, (part + 1) * TILES * D // 2)
                nc.sync.dma_start(out=resident[:, 0, columns], in_=rows[0][:, columns])

        load_first_chunk(attn_rows, attn_all)
        merge_words_given, merge_plane_given = load_weight(nc, keep, W_merge_words, W_merge_scales, "merge_given")
        load_first_chunk(x_rows, x_all)
        for c in range(1, NORM_LAG + 1):
            load_chunk(attn_rows, attn_all, c)
            load_chunk(x_rows, x_all, c)
        w1_words, w1_plane = load_weight(nc, keep, W1_words, W1_scales, "w1")
        for c in range(NORM_LAG + 1, N_CHUNKS):
            load_chunk(attn_rows, attn_all, c)
            load_chunk(x_rows, x_all, c)

        merge_words = keep.tile([P, D], U32, align_bytes=64)
        nc.vector.tensor_copy(
            out=merge_words[:].bitcast(I32).rearrange("p (t m) -> p t m", t=PACK),
            in_=merge_words_given[:].bitcast(I32).rearrange("p (m t) -> p t m", t=PACK),
        )
        merge_plane = keep.tile([P, D], U8, align_bytes=64)
        nc.vector.tensor_copy(
            out=merge_plane[:].rearrange("p (t m) -> p m t", t=PACK),
            in_=merge_plane_given[:].rearrange("p (m t) -> p m t", t=PACK),
        )

        one = keep.tile([P, 1], F32)
        nc.vector.memset(one[:], 1.0)
        nc.scalar.sqrt(out=one[:], in_=one[:])

        ones = keep.tile([P, P], BF16)
        nc.vector.memset(ones[:], 1.0)
        b1_padded = keep.tile([P, D], BF16)
        nc.vector.memset(b1_padded[:], 0.0)
        nc.scalar.dma_start(out=b1_padded[0:1, :], in_=b1.unsqueeze(0))
        b1_summed = product_pool.tile([P, D], F32, name="product")
        nc.tensor.matmul(out=b1_summed[:], lhsT=ones[:], rhs=b1_padded[:], start=True, stop=True)
        b1_rows = keep.tile([P, D], F32)
        nc.scalar.copy(out=b1_rows[:], in_=b1_summed[:])
        b_merge_pt = keep.tile([P, PACK], BF16)
        nc.scalar.dma_start(out=b_merge_pt[:], in_=b_merge.rearrange("(p t) -> p t", t=PACK))
        gamma_pt = keep.tile([P, PACK], BF16)
        nc.scalar.dma_start(out=gamma_pt[:], in_=gamma2.rearrange("a b (p t) -> (a b p) t", t=PACK))
        beta_pt = keep.tile([P, PACK], BF16)
        nc.scalar.dma_start(out=beta_pt[:], in_=beta2.rearrange("a b (p t) -> (a b p) t", t=PACK))

        identity = keep.tile([P, P], F32)
        make_identity(nc, identity[:])

        attn_mx = {}
        xn_mx = {}
        x_turned = {}
        x2_t_of_batch = {}
        sums_of_batch = {}
        squares_of_batch = {}
        mean_terms_of_batch = {}
        norm_of_batch = {}

        def chunk_columns(c):
            half = c % HALVES
            return slice(half * TILES * D, (half + 1) * TILES * D)

        def turn(resident, c, label):
            pairs = resident[:, c, :].bitcast(F32)
            grouped = work.tile([P, CHUNK * PACK], BF16, name=label + "_grouped", align_bytes=64)
            grouped_pairs = grouped[:].bitcast(F32).rearrange("p (i w u) -> p i w u", i=TILES, u=2)

            def turn_two(two):
                turned = turned_pool.tile([P, 2, 2, P], F32)
                for j in range(2):
                    first = (2 * two + j) * (D // 2)
                    for u in range(2):
                        nc.tensor.transpose(turned[:, j, u, :], pairs[:, first + u : first + D // 2 : 2], identity[:])
                nc.scalar.copy(
                    out=grouped_pairs[:, 2 * two : 2 * two + 2], in_=turned[:].rearrange("p j u w -> p j w u")
                )

            return grouped, turn_two

        def quantise(grouped, label):
            codes = work.tile([P, CHUNK], U32, name=label + "_codes", align_bytes=64)
            plane = work.tile([P, CHUNK], U8, name=label + "_plane", align_bytes=64)
            nc.vector.quantize_mx(out=codes[:].bitcast(FP8X4), scales=plane[:], in_=grouped)
            return codes, plane

        def merge(c):
            batch, half = divmod(c, HALVES)
            if half == 0:
                x2_t_all = work.tile([P, PACK, TOKENS], F32)
                x2_t_of_batch[batch] = x2_t_all
                sums = work.tile([P, PACK, HALVES], F32)
                sums_of_batch[batch] = sums
                square_terms = work.tile([P, PACK, HALVES + 1], F32)
                squares_of_batch[batch] = square_terms
            codes, plane = attn_mx[c]
            x_by_slab = x_turned[c][:].rearrange("p (w t) -> p t w", t=PACK)

            def merge_slab(t):
                slab = slice(t * P, (t + 1) * P)
                product = product_pool.tile([P, CHUNK], F32)
                nc.tensor.matmul_mx(
                    out=product[:],
                    lhsT=merge_words[:, slab].bitcast(FP8X4),
                    lhsT_scale=merge_plane[:, slab],
                    rhs=codes[:].bitcast(FP8X4),
                    rhs_scale=plane[:],
                    start=True,
                    stop=True,
                )
                nc.vector.scalar_tensor_tensor(
                    out=x2_t_of_batch[batch][:, t, half * CHUNK : (half + 1) * CHUNK],
                    in0=product[:],
                    scalar=b_merge_pt[:, t : t + 1],
                    in1=x_by_slab[:, t, :],
                    op0=ALU.add,
                    op1=ALU.add,
                    accum_out=sums_of_batch[batch][:, t, half : half + 1],
                )

            return merge_slab

        def square_sums(c):
            batch, half = divmod(c, HALVES)
            for t in range(PACK):
                squares = work.tile([P, CHUNK], BF16, bufs=4)
                nc.scalar.activation(
                    out=squares[:],
                    in_=x2_t_of_batch[batch][:, t, half * CHUNK : (half + 1) * CHUNK],
                    func=ACT.Square,
                    accum_out=squares_of_batch[batch][:, t, half : half + 1],
                )

        def turn_back(c):
            batch, half = divmod(c, HALVES)
            x2 = work.tile([P, TILES, D], F32, bufs=3)

            def turn_back_tile(i):
                x2_back = turned_pool.tile([P, PACK, P], F32, name="turned")
                first = half * CHUNK + i * P
                for t in range(PACK):
                    nc.tensor.transpose(x2_back[:, t, :], x2_t_of_batch[batch][:, t, first : first + P], identity[:])
                copier = nc.vector.tensor_copy if batch == 0 and i < TILES // 2 else nc.scalar.copy
                copier(out=x2[:, i, :].rearrange("p (m t) -> p m t", t=PACK), in_=x2_back[:].rearrange("p t m -> p m t"))
                if i == TILES - 1:
                    nc.sync.dma_start(out=x2_rows[batch][:, chunk_columns(c)], in_=x2[:].rearrange("p i n -> p (i n)"))

            return turn_back_tile

        def mean_terms(batch):
            total = work.tile([P, PACK], F32)
            nc.vector.tensor_reduce(out=total[:], in_=sums_of_batch[batch][:], axis=AXIS.X, op=ALU.add)
            nc.vector.scalar_tensor_tensor(
                out=squares_of_batch[batch][:, :, HALVES],
                in0=total[:],
                scalar=-1.0 / TOKENS,
                in1=total[:],
                op0=ALU.mult,
                op1=ALU.mult,
            )
            minus_mean_gamma = work.tile([P, PACK], F32)
            nc.vector.scalar_tensor_tensor(
                out=minus_mean_gamma[:], in0=total[:], scalar=-1.0 / TOKENS, in1=gamma_pt[:], op0=ALU.mult, op1=ALU.mult
            )
            mean_terms_of_batch[batch] = minus_mean_gamma

        def norm_coefficients(batch):
            spread = work.tile([P, PACK], F32)
            nc.vector.tensor_reduce(out=spread[:], in_=squares_of_batch[batch][:], axis=AXIS.X, op=ALU.add)
            std = work.tile([P, PACK], F32)
            nc.scalar.activation(out=std[:], in_=spread[:], func=ACT.Sqrt, scale=1.0 / TOKENS, bias=EPS)
            rstd = work.tile([P, PACK], F32)
            nc.vector.reciprocal(rstd[:], std[:])
            minus_mean_gain = work.tile([P, PACK], F32)
            nc.vector.tensor_mul(minus_mean_gain[:], mean_terms_of_batch[batch][:], rstd[:])
            gain = work.tile([P, PACK], F32)
            nc.vector.tensor_mul(gain[:], gamma_pt[:], rstd[:])
            shift = work.tile([P, PACK], F32)
            nc.vector.tensor_add(shift[:], minus_mean_gain[:], beta_pt[:])
            norm_of_batch[batch] = (gain, shift)

        def normalise(c):
            batch, half = divmod(c, HALVES)
            gain, shift = norm_of_batch[batch]
            xn_slabs = work.tile([P, PACK, CHUNK], BF16)
            for t in range(PACK):
                x2_t_slab = x2_t_of_batch[batch][:, t, half * CHUNK : (half + 1) * CHUNK]
                if t < SCALAR_SLABS:
                    nc.scalar.activation(
                        out=xn_slabs[:, t, :],
                        in_=x2_t_slab,
                        func=ACT.Identity,
                        scale=gain[:, t : t + 1],
                        bias=shift[:, t : t + 1],
                    )
                else:
                    nc.vector.tensor_scalar(
                        out=xn_slabs[:, t, :],
                        in0=x2_t_slab,
                        scalar1=gain[:, t : t + 1],
                        scalar2=shift[:, t : t + 1],
                        op0=ALU.mult,
                        op1=ALU.add,
                    )
            xn_grouped = work.tile([P, CHUNK, PACK], BF16, align_bytes=64)
            nc.vector.tensor_copy(
                out=xn_grouped[:].rearrange("p (c i) t -> p c t i", i=RUN),
                in_=xn_slabs[:].rearrange("p t (c i) -> p c t i", i=RUN),
            )
            return xn_grouped

        def expand(c):
            codes, plane = xn_mx[c]
            ffh = work.tile([P, TILES, D], F32, bufs=3)

            def expand_tile(i):
                tokens = slice(i * P, (i + 1) * P)
                product = product_pool.tile([P, D], F32)
                nc.tensor.matmul_mx(
                    out=product[:],
                    lhsT=codes[:, tokens].bitcast(FP8X4),
                    lhsT_scale=plane[:, tokens],
                    rhs=w1_words[:].bitcast(FP8X4),
                    rhs_scale=w1_plane[:],
                    start=True,
                    stop=True,
                )
                nc.vector.tensor_tensor(out=ffh[:, i, :], in0=product[:], in1=b1_rows[:], op=ALU.add)
                together = 1 if c == N_CHUNKS - 1 else 2
                if (i + 1) % together == 0:
                    first = ((c % HALVES) * TILES + i + 1 - together) * D
                    nc.sync.dma_start(
                        out=ffh_rows[c // HALVES][:, first : first + together * D],
                        in_=ffh[:, i + 1 - together : i + 1, :].rearrange("p i n -> p (i n)"),
                    )

            return expand_tile

        chunks = range(N_CHUNKS)
        with tc.manual_schedule(engines={mybir.EngineType.PE}):
            for step in range(-1, N_CHUNKS + NORM_LAG + 1):
                ahead, back, normed, expanded = step + 1, step - 1, step - NORM_LAG, step - NORM_LAG - 1
                if normed in chunks and normed % HALVES == 0:
                    norm_coefficients(normed // HALVES)
                if step in chunks:
                    merge_slab = merge(step)
                    merge_slab(0)
                    merge_slab(1)
                if ahead in chunks:
                    attn_grouped, turn_two = turn(attn_all, ahead, "attn")
                    turn_two(0)
                    turn_two(1)
                if normed in chunks:
                    xn_grouped = normalise(normed)
                if step in chunks:
                    merge_slab(2)
                    merge_slab(3)
                    if step % HALVES == HALVES - 1:
                        mean_terms(step // HALVES)
                if ahead in chunks:
                    x_turned[ahead], turn_two = turn(x_all, ahead, "x")
                    turn_two(0)
                    turn_two(1)
                    attn_mx[ahead] = quantise(attn_grouped[:], "attn")
                if expanded in chunks:
                    expand_tile = expand(expanded)
                    expand_tile(0)
                    expand_tile(1)
                if normed in chunks:
                    xn_mx[normed] = quantise(xn_grouped[:].rearrange("p w t -> p (w t)"), "xn")
                if back in chunks:
                    turn_back_tile = turn_back(back)
                    turn_back_tile(0)
                    turn_back_tile(1)
                if expanded in chunks:
                    expand_tile(2)
                    expand_tile(3)
                if back in chunks:
                    turn_back_tile(2)
                    turn_back_tile(3)
                if step in chunks:
                    square_sums(step)
